import numpy as np
import ml_dtypes


def mxq(x, axis, fmt="e4m3"):
    dtype, down = {"e4m3": (ml_dtypes.float8_e4m3fn, 7), "e5m2": (ml_dtypes.float8_e5m2, 14)}[fmt]
    v = np.moveaxis(np.asarray(x, np.float32).astype(ml_dtypes.bfloat16).astype(np.float64), axis, -1)
    blocks = v.reshape(v.shape[:-1] + (-1, 32))
    amax = np.abs(blocks).max(-1, keepdims=True)
    byte = np.maximum(np.where(amax > 0, np.frexp(amax)[1] - 1 + 127, 0) - down, 1)
    scale = np.exp2(byte - 127.0)
    codes = (blocks / scale).astype(np.float32).astype(dtype).astype(np.float64)
    return np.moveaxis((codes * scale).reshape(v.shape), -1, axis)


WIDE = False


def mx_kscale(k):
    if not WIDE:
        return np.ones(k)
    levels = np.array([10, -10, 5, -5, 0])
    a = np.random.permutation(np.resize(levels, k // 512 * 4)).reshape(k // 512, 4)
    idx = np.arange(k)
    return np.exp2(a[idx // 512, idx % 128 // 32])


BF16 = ml_dtypes.bfloat16


def bf(x):
    return np.asarray(x, np.float32).astype(BF16)


def f64(x):
    return np.asarray(x).astype(np.float64)


E2M1 = np.array([0.0, 0.5, 1.0, 1.5, 2.0, 3.0, 4.0, 6.0, -0.0, -0.5, -1.0, -1.5, -2.0, -3.0, -4.0, -6.0])


def pack_weight(w, fmt):
    k, n = w.shape
    w = f64(bf(w)).reshape(k // 32, 32, n)
    amax = np.abs(w).max(1)
    if fmt == "e4m3":
        byte = np.frexp(amax)[1] - 1 + 127 - 7
    else:
        mant, ex = np.frexp(amax / 6.0)
        byte = np.where(mant > 0.5, ex, ex - 1) + 127
    byte = np.clip(np.where(amax > 0, byte, 1), 1, 254)
    scaled = (w * np.exp2(127.0 - byte)[:, None, :]).reshape(k, n).astype(np.float32)
    by_word = np.ascontiguousarray(scaled.reshape(k // 512, 128, 4, n).transpose(0, 1, 3, 2))
    if fmt == "e4m3":
        words = by_word.astype(ml_dtypes.float8_e4m3fn).view(np.uint8)
    else:
        c = by_word.astype(ml_dtypes.float4_e2m1fn).view(np.uint8) & 0xF
        words = c[..., 0::2] | (c[..., 1::2] << 4)
    return np.ascontiguousarray(words), np.ascontiguousarray(byte.astype(np.uint8).reshape(k // 512, 16, n))


def unpack_weight(words, scales, fmt):
    g, p, n, _ = words.shape
    if fmt == "e4m3":
        vals = np.ascontiguousarray(words).view(ml_dtypes.float8_e4m3fn).astype(np.float64)
    else:
        nib = np.empty((g, p, n, 4), np.uint8)
        nib[..., 0::2] = words & 0xF
        nib[..., 1::2] = words >> 4
        vals = E2M1[nib]
    vals = vals * np.repeat(np.exp2(scales.astype(np.float64) - 127.0), 8, axis=1)[..., None]
    return vals.transpose(0, 1, 3, 2).reshape(g * 512, n)


B, HD, NH, H, W, F = 2, 1024, 8, 16, 32, 2048
HEAD = HD // NH
P = H * W


def rms_in(x, w, eps=1e-8):
    std = np.std(x, axis=(-2, -1), keepdims=True, ddof=1)
    return x / (std + eps) * w[None, :, None, None]


def ln(x, w, b, eps=1e-5):
    mu = np.mean(x, axis=-1, keepdims=True)
    var = np.var(x, axis=-1, keepdims=True)
    return (x - mu) / np.sqrt(var + eps) * w + b


def setup_inputs():
    n = np.random.standard_normal
    s = mx_kscale(HD)
    x = bf(n((B, HD, H, W)) * (0.5 + np.random.random((B, HD, 1, 1))) + 0.5 * n((B, HD, 1, 1)))
    norm1_w = bf((1.0 + 0.1 * n(HD)) * s)
    qkv_w = n((3 * HD, HD)) / np.sqrt(HD) / s[None, :]
    qkv_w_words, qkv_w_scales = pack_weight(np.ascontiguousarray(qkv_w.T), "e4m3")
    return {"x": x,
            "norm1_w": norm1_w,
            "qkv_w_words": qkv_w_words,
            "qkv_w_scales": qkv_w_scales,
            "qkv_b": bf(0.1 * n(3 * HD)),
            "qn_w": bf(1.0 + 0.1 * n(HEAD)), "qn_b": bf(0.1 * n(HEAD)),
            "kn_w": bf(1.0 + 0.1 * n(HEAD)), "kn_b": bf(0.1 * n(HEAD))}


def reference(x, norm1_w, qkv_w_words, qkv_w_scales, qkv_b, qn_w, qn_b, kn_w, kn_b):
    h1 = rms_in(f64(x), f64(norm1_w)).reshape(B, HD, P)
    qkv = (unpack_weight(qkv_w_words, qkv_w_scales, "e4m3").T @ mxq(h1, 1, "e4m3")) + f64(qkv_b)[None, :, None]
    t = qkv.reshape(B, NH, 3 * HEAD, H, W).transpose(0, 1, 3, 4, 2)
    q, k, v = np.split(t, 3, axis=-1)
    q = ln(q, f64(qn_w), f64(qn_b))
    k = ln(k, f64(kn_w), f64(kn_b))
    return q, k, np.ascontiguousarray(v)

@@ -1,0 +1,243 @@
+from contextlib import ExitStack
+
+import concourse.mybir as mybir
+
+F32 = mybir.dt.float32
+BF16 = mybir.dt.bfloat16
+I32 = mybir.dt.int32
+U32 = mybir.dt.uint32
+U8 = mybir.dt.uint8
+FP8X4 = mybir.dt.float8_e4m3fn_x4
+ALU = mybir.AluOpType
+ACT = mybir.ActivationFunctionType
+
+P = 128
+PACK = 4
+PASSES = 2
+BATCH = 2
+POS = 512
+POS_TILES = POS // P
+HEADS = 8
+HEAD = 128
+OUT = HEADS * 3 * HEAD
+ROWS = PASSES * PACK
+QK = 2
+GROUPS = [(s, t) for s in range(QK) for t in range(POS_TILES)]
+UNITS = BATCH * HEADS
+PREPARE_STEP = 3
+
+FLOPS = 2 * BATCH * POS * (PASSES * P * PACK) * OUT
+
+
+def tile_axialattentionblock_pa_kernel(
+    tc, x, norm1_w, qkv_w_words, qkv_w_scales, qkv_b, qn_w, qn_b, kn_w, kn_b, out_0, out_1, out_2
+):
+    nc = tc.nc
+    with ExitStack() as stack:
+        keep = stack.enter_context(tc.tile_pool(name="keep", bufs=1))
+        stage = stack.enter_context(tc.tile_pool(name="stage", bufs=2))
+        small = stack.enter_context(tc.tile_pool(name="small", bufs=4))
+        work = stack.enter_context(tc.tile_pool(name="work", bufs=3))
+        psum = stack.enter_context(tc.psum_pool(name="psum", bufs=2))
+        const_psum = stack.enter_context(tc.psum_pool(name="const_psum", bufs=1))
+        stack.enter_context(tc.manual_schedule())
+
+        x_rows = x.rearrange("b (g p j) h w -> b g p (j h w)", g=PASSES, p=P, j=PACK)
+        x_sb = [keep.tile([P, PASSES, PACK * POS], BF16, name="x_sb%d" % b) for b in range(BATCH)]
+        for g in range(PASSES):
+            nc.sync.dma_start(out=x_sb[0][:, g, :], in_=x_rows[0, g])
+
+        w_planes = keep.tile([P, PASSES, OUT], U8, align_bytes=64)
+        nc.vector.memset(w_planes[:].bitcast(I32), 0)
+        scale_rows = qkv_w_scales.rearrange("g (i a r) n -> a r i g n", i=2, a=2, r=4)
+        for a in range(2):
+            for r in range(4):
+                nc.sync.dma_start(
+                    out=w_planes[32 * a + r : P : 64].bitcast(I32), in_=scale_rows[a, r].bitcast(I32)
+                )
+
+        w_words = keep.tile([P, PASSES, OUT], U32, align_bytes=64)
+        words_dram = qkv_w_words.rearrange("g p n t -> p g (n t)")
+        chunk = 2 * 3 * HEAD
+        for c0 in range(0, OUT, chunk):
+            nc.sync.dma_start(
+                out=w_words[:, :, c0 : c0 + chunk].bitcast(I32),
+                in_=words_dram[:, :, PACK * c0 : PACK * (c0 + chunk)].bitcast(I32),
+            )
+        for g in range(PASSES):
+            nc.sync.dma_start(out=x_sb[1][:, g, :], in_=x_rows[1, g])
+
+        w1 = keep.tile([P, ROWS], BF16)
+        nc.scalar.dma_start(
+            out=w1[:].rearrange("p (g j) -> p g j", g=PASSES),
+            in_=norm1_w.rearrange("(g p j) -> p g j", g=PASSES, p=P, j=PACK),
+        )
+        bias = keep.tile([P, HEADS, 3, HEAD], BF16)
+        nc.scalar.dma_start(out=bias[:].rearrange("p n s c -> p (n s c)"), in_=qkv_b.partition_broadcast(P))
+        ln_rows = keep.tile([P, 2, QK, HEAD], BF16)
+        nc.vector.memset(ln_rows[:], 0.0)
+        for s, (w_vec, b_vec) in enumerate(((qn_w, qn_b), (kn_w, kn_b))):
+            nc.scalar.dma_start(out=ln_rows[0:1, 0, s, :], in_=w_vec.unsqueeze(0))
+            nc.scalar.dma_start(out=ln_rows[0:1, 1, s, :], in_=b_vec.unsqueeze(0))
+        ones = keep.tile([P, P], BF16)
+        nc.vector.memset(ones[:], 1.0)
+        ln_eps = keep.tile([P, 1], F32)
+        nc.vector.memset(ln_eps[:], 1e-5)
+        ln_bank = const_psum.tile([P, 2, QK, HEAD], F32)
+        nc.tensor.matmul(
+            out=ln_bank[:].rearrange("p a s c -> p (a s c)"), lhsT=ones[:],
+            rhs=ln_rows[:].rearrange("p a s c -> p (a s c)"), start=True, stop=True,
+        )
+        gain = ln_bank[:, 0]
+        shift = ln_bank[:, 1]
+
+        h_codes = [keep.tile([P, PASSES, POS], U32, name="h_codes%d" % b, align_bytes=64) for b in range(BATCH)]
+        h_planes = [keep.tile([P, PASSES, POS], U8, name="h_planes%d" % b, align_bytes=64) for b in range(BATCH)]
+        mean_var = [keep.tile([P, ROWS, 2], F32, name="mean_var%d" % b) for b in range(BATCH)]
+
+        def image_statistics(b):
+            stats = small.tile([P, ROWS, 6], F32)
+            for row in range(ROWS):
+                nc.vector.bn_stats(out=stats[:, row, :], in_=x_sb[b][:, row // PACK, (row % PACK) * POS : (row % PACK + 1) * POS])
+            for row in range(ROWS):
+                nc.vector.bn_aggr(out=mean_var[b][:, row, :], in_=stats[:, row, :])
+
+        def quantise_image(b):
+            std = small.tile([P, ROWS], F32)
+            nc.scalar.activation(out=std[:], in_=mean_var[b][:, :, 1], func=ACT.Sqrt, scale=POS / (POS - 1.0))
+            padded = small.tile([P, ROWS], F32)
+            nc.vector.tensor_scalar_add(out=padded[:], in0=std[:], scalar1=1e-8)
+            recip = small.tile([P, ROWS], F32)
+            nc.vector.reciprocal(out=recip[:], in_=padded[:])
+            factor = small.tile([P, ROWS], F32)
+            nc.vector.tensor_tensor(out=factor[:], in0=recip[:], in1=w1[:], op=ALU.mult)
+            grouped = []
+            for g in range(PASSES):
+                grouped.append(stage.tile([P, POS, PACK], BF16, name="grouped%d" % g, align_bytes=64))
+                nc.vector.tensor_tensor(
+                    out=grouped[g][:].rearrange("p (t m) j -> p t m j", t=POS_TILES),
+                    in0=x_sb[b][:, g, :].rearrange("p (j m t) -> p t m j", j=PACK, t=POS_TILES),
+                    in1=factor[:, g * PACK : (g + 1) * PACK].unsqueeze(1).unsqueeze(1).to_broadcast([P, POS_TILES, P, PACK]),
+                    op=ALU.mult,
+                )
+            for g in range(PASSES):
+                nc.vector.quantize_mx(
+                    out=h_codes[b][:, g, :].bitcast(FP8X4),
+                    scales=h_planes[b][:, g, :],
+                    in_=grouped[g][:].rearrange("p c j -> p (c j)"),
+                )
+
+        def dram_head(out, n):
+            return out.rearrange("b n y x c -> (b n) (y x c)")[n].rearrange("(m f) -> m f", m=P)
+
+        tiles = {}
+
+        def project(n):
+            b, h = divmod(n, HEADS)
+            c0 = h * 3 * HEAD
+            for a in range(2):
+                tiles["qk_bank%d" % a, n] = psum.tile([P, 2, QK, HEAD], F32, name="qk_bank%d" % a)
+            tiles["v_bank", n] = psum.tile([P, POS_TILES, HEAD], F32, name="v_bank")
+            for t in range(POS_TILES):
+                rows = slice(t * P, (t + 1) * P)
+                for acc, cols in (
+                    (tiles["qk_bank%d" % (t // 2), n][:, t % 2].rearrange("p s c -> p (s c)"), slice(c0, c0 + QK * HEAD)),
+                    (tiles["v_bank", n][:, t, :], slice(c0 + QK * HEAD, c0 + 3 * HEAD)),
+                ):
+                    for g in range(PASSES):
+                        nc.tensor.matmul_mx(
+                            out=acc,
+                            lhsT=h_codes[b][:, g, rows].bitcast(FP8X4),
+                            lhsT_scale=h_planes[b][:, g, rows],
+                            rhs=w_words[:, g, cols].bitcast(FP8X4),
+                            rhs_scale=w_planes[:, g, cols],
+                            start=(g == 0),
+                            stop=(g == PASSES - 1),
+                        )
+
+        def leave_psum(n):
+            h = n % HEADS
+            v_out = work.tile([P, POS_TILES, HEAD], F32)
+            nc.vector.tensor_tensor(
+                out=v_out[:], in0=tiles["v_bank", n][:],
+                in1=bias[:, h, 2, :].unsqueeze(1).to_broadcast([P, POS_TILES, HEAD]), op=ALU.add,
+            )
+            nc.sync.dma_start(out=dram_head(out_2, n), in_=v_out[:].rearrange("p t c -> p (t c)"))
+            y = work.tile([P, QK, POS_TILES, HEAD], F32)
+            sum_y = small.tile([P, QK, POS_TILES], F32)
+            for s, t in GROUPS:
+                nc.scalar.activation(
+                    out=y[:, s, t, :], in_=tiles["qk_bank%d" % (t // 2), n][:, t % 2, s, :], func=ACT.Identity,
+                    accum_out=sum_y[:, s, t : t + 1],
+                )
+            neg_mean = small.tile([P, QK, POS_TILES], F32)
+            nc.vector.scalar_tensor_tensor(
+                out=neg_mean[:], in0=sum_y[:], scalar=-1.0 / HEAD,
+                in1=neg_bias_mean[:, h, :].unsqueeze(2).to_broadcast([P, QK, POS_TILES]),
+                op0=ALU.mult, op1=ALU.add,
+            )
+            u = work.tile([P, QK, POS_TILES, HEAD], F32)
+            nc.gpsimd.tensor_tensor(
+                out=u[:], in0=y[:],
+                in1=bias[:, h, 0:QK, :].unsqueeze(2).to_broadcast([P, QK, POS_TILES, HEAD]), op=ALU.add,
+            )
+            tiles["u", n] = u
+            tiles["neg_mean", n] = neg_mean
+
+        def centre(n):
+            u = tiles["u", n]
+            neg_mean = tiles["neg_mean", n]
+            unread = work.tile([P, QK, POS_TILES, HEAD], BF16)
+            sum_sq = small.tile([P, QK, POS_TILES], F32)
+            for s, t in GROUPS:
+                nc.scalar.activation(
+                    out=unread[:, s, t, :], in_=u[:, s, t, :], func=ACT.Square,
+                    bias=neg_mean[:, s, t : t + 1], accum_out=sum_sq[:, s, t : t + 1],
+                )
+            ln_std = small.tile([P, QK, POS_TILES], F32)
+            nc.scalar.activation(out=ln_std[:], in_=sum_sq[:], func=ACT.Sqrt, scale=1.0 / HEAD, bias=ln_eps[:, 0:1])
+            centred = work.tile([P, QK, POS_TILES, HEAD], F32)
+            for s, t in GROUPS:
+                nc.vector.scalar_tensor_tensor(
+                    out=centred[:, s, t, :], in0=u[:, s, t, :], scalar=neg_mean[:, s, t : t + 1],
+                    in1=gain[:, s, :], op0=ALU.add, op1=ALU.mult,
+                )
+            tiles["ln_std", n] = ln_std
+            tiles["centred", n] = centred
+
+        def finish(n):
+            rstd = small.tile([P, QK, POS_TILES], F32)
+            nc.vector.reciprocal(out=rstd[:], in_=tiles["ln_std", n][:])
+            qk_out = work.tile([P, QK, POS_TILES, HEAD], F32)
+            for s, t in GROUPS:
+                nc.vector.scalar_tensor_tensor(
+                    out=qk_out[:, s, t, :], in0=tiles["centred", n][:, s, t, :], scalar=rstd[:, s, t : t + 1],
+                    in1=shift[:, s, :], op0=ALU.mult, op1=ALU.add,
+                )
+            for s, out in enumerate((out_0, out_1)):
+                nc.sync.dma_start(out=dram_head(out, n), in_=qk_out[:, s].rearrange("p t c -> p (t c)"))
+
+        image_statistics(0)
+        neg_bias_mean = keep.tile([P, HEADS, QK], F32)
+        bias_unread = keep.tile([P, HEADS, QK, HEAD], BF16)
+        for h in range(HEADS):
+            for s in range(QK):
+                nc.scalar.activation(
+                    out=bias_unread[:, h, s, :], in_=bias[:, h, s, :], func=ACT.Identity,
+                    scale=-1.0 / HEAD, accum_out=neg_bias_mean[:, h, s : s + 1],
+                )
+        quantise_image(0)
+        project(0)
+        for step in range(UNITS + 2):
+            if step == PREPARE_STEP:
+                image_statistics(1)
+            if step == PREPARE_STEP + 1:
+                quantise_image(1)
+            if step + 1 < UNITS:
+                project(step + 1)
+            if step < UNITS:
+                leave_psum(step)
+            if 1 <= step <= UNITS:
+                centre(step - 1)
+            if step >= 2:
+                finish(step - 2)

@@ -24,7 +24,7 @@ ROWS = PASSES * PACK
 QK = 2
 GROUPS = [(s, t) for s in range(QK) for t in range(POS_TILES)]
 UNITS = BATCH * HEADS
-PREPARE_STEP = 3
+QUANTISE_STEP = 2
 
 FLOPS = 2 * BATCH * POS * (PASSES * P * PACK) * OUT
 
@@ -36,7 +36,7 @@ def tile_axialattentionblock_pa_kernel(
     with ExitStack() as stack:
         keep = stack.enter_context(tc.tile_pool(name="keep", bufs=1))
         stage = stack.enter_context(tc.tile_pool(name="stage", bufs=2))
-        small = stack.enter_context(tc.tile_pool(name="small", bufs=4))
+        small = stack.enter_context(tc.tile_pool(name="small", bufs=6))
         work = stack.enter_context(tc.tile_pool(name="work", bufs=3))
         psum = stack.enter_context(tc.psum_pool(name="psum", bufs=2))
         const_psum = stack.enter_context(tc.psum_pool(name="const_psum", bufs=1))
@@ -137,7 +137,7 @@ def tile_axialattentionblock_pa_kernel(
             c0 = h * 3 * HEAD
             for a in range(2):
                 tiles["qk_bank%d" % a, n] = psum.tile([P, 2, QK, HEAD], F32, name="qk_bank%d" % a)
-            tiles["v_bank", n] = psum.tile([P, POS_TILES, HEAD], F32, name="v_bank")
+            tiles["v_bank", n] = psum.tile([P, POS_TILES, HEAD], F32, name="v_bank", bufs=3)
             for t in range(POS_TILES):
                 rows = slice(t * P, (t + 1) * P)
                 for acc, cols in (
@@ -171,12 +171,12 @@ def tile_axialattentionblock_pa_kernel(
                     accum_out=sum_y[:, s, t : t + 1],
                 )
             neg_mean = small.tile([P, QK, POS_TILES], F32)
-            nc.vector.scalar_tensor_tensor(
-                out=neg_mean[:], in0=sum_y[:], scalar=-1.0 / HEAD,
-                in1=neg_bias_mean[:, h, :].unsqueeze(2).to_broadcast([P, QK, POS_TILES]),
-                op0=ALU.mult, op1=ALU.add,
-            )
-            u = work.tile([P, QK, POS_TILES, HEAD], F32)
+            for s in range(QK):
+                nc.gpsimd.tensor_scalar(
+                    out=neg_mean[:, s, :], in0=sum_y[:, s, :], scalar1=-1.0 / HEAD,
+                    scalar2=neg_bias_mean[:, h, s : s + 1], op0=ALU.mult, op1=ALU.add,
+                )
+            u = work.tile([P, QK, POS_TILES, HEAD], F32, bufs=5)
             nc.gpsimd.tensor_tensor(
                 out=u[:], in0=y[:],
                 in1=bias[:, h, 0:QK, :].unsqueeze(2).to_broadcast([P, QK, POS_TILES, HEAD]), op=ALU.add,
@@ -228,16 +228,15 @@ def tile_axialattentionblock_pa_kernel(
                 )
         quantise_image(0)
         project(0)
-        for step in range(UNITS + 2):
-            if step == PREPARE_STEP:
-                image_statistics(1)
-            if step == PREPARE_STEP + 1:
+        image_statistics(1)
+        for step in range(UNITS + 3):
+            if step == QUANTISE_STEP:
                 quantise_image(1)
             if step + 1 < UNITS:
                 project(step + 1)
             if step < UNITS:
                 leave_psum(step)
-            if 1 <= step <= UNITS:
-                centre(step - 1)
-            if step >= 2:
-                finish(step - 2)
+            if 0 <= step - 2 < UNITS:
+                centre(step - 2)
+            if step >= 3:
+                finish(step - 3)

@@ -24,7 +24,6 @@ ROWS = PASSES * PACK
 QK = 2
 GROUPS = [(s, t) for s in range(QK) for t in range(POS_TILES)]
 UNITS = BATCH * HEADS
-QUANTISE_STEP = 2
 
 FLOPS = 2 * BATCH * POS * (PASSES * P * PACK) * OUT
 
@@ -44,8 +43,9 @@ def tile_axialattentionblock_pa_kernel(
 
         x_rows = x.rearrange("b (g p j) h w -> b g p (j h w)", g=PASSES, p=P, j=PACK)
         x_sb = [keep.tile([P, PASSES, PACK * POS], BF16, name="x_sb%d" % b) for b in range(BATCH)]
-        for g in range(PASSES):
-            nc.sync.dma_start(out=x_sb[0][:, g, :], in_=x_rows[0, g])
+        for b in range(BATCH):
+            for g in range(PASSES):
+                nc.sync.dma_start(out=x_sb[b][:, g, :], in_=x_rows[b, g])
 
         w_planes = keep.tile([P, PASSES, OUT], U8, align_bytes=64)
         nc.vector.memset(w_planes[:].bitcast(I32), 0)
@@ -64,8 +64,6 @@ def tile_axialattentionblock_pa_kernel(
                 out=w_words[:, :, c0 : c0 + chunk].bitcast(I32),
                 in_=words_dram[:, :, PACK * c0 : PACK * (c0 + chunk)].bitcast(I32),
             )
-        for g in range(PASSES):
-            nc.sync.dma_start(out=x_sb[1][:, g, :], in_=x_rows[1, g])
 
         w1 = keep.tile([P, ROWS], BF16)
         nc.scalar.dma_start(
@@ -93,18 +91,34 @@ def tile_axialattentionblock_pa_kernel(
 
         h_codes = [keep.tile([P, PASSES, POS], U32, name="h_codes%d" % b, align_bytes=64) for b in range(BATCH)]
         h_planes = [keep.tile([P, PASSES, POS], U8, name="h_planes%d" % b, align_bytes=64) for b in range(BATCH)]
-        mean_var = [keep.tile([P, ROWS, 2], F32, name="mean_var%d" % b) for b in range(BATCH)]
+        mean_var = [keep.tile([P, PACK, 2], F32, name="mean_var%d" % b) for b in range(BATCH)]
+        x_sum_sq = [keep.tile([P, PACK], F32, name="x_sum_sq%d" % b) for b in range(BATCH)]
 
-        def image_statistics(b):
-            stats = small.tile([P, ROWS, 6], F32)
-            for row in range(ROWS):
-                nc.vector.bn_stats(out=stats[:, row, :], in_=x_sb[b][:, row // PACK, (row % PACK) * POS : (row % PACK + 1) * POS])
-            for row in range(ROWS):
-                nc.vector.bn_aggr(out=mean_var[b][:, row, :], in_=stats[:, row, :])
+        def statistics_on_vector(b):
+            stats = small.tile([P, PACK, 6], F32)
+            for j in range(PACK):
+                nc.vector.bn_stats(out=stats[:, j, :], in_=x_sb[b][:, 0, j * POS : (j + 1) * POS])
+            for j in range(PACK):
+                nc.vector.bn_aggr(out=mean_var[b][:, j, :], in_=stats[:, j, :])
+
+        def statistics_on_scalar(b):
+            x_unread = stage.tile([P, 2, PACK, POS], BF16)
+            x_neg_mean = small.tile([P, PACK], F32)
+            for j in range(PACK):
+                nc.scalar.activation(
+                    out=x_unread[:, 0, j, :], in_=x_sb[b][:, 1, j * POS : (j + 1) * POS], func=ACT.Identity,
+                    scale=-1.0 / POS, accum_out=x_neg_mean[:, j : j + 1],
+                )
+            for j in range(PACK):
+                nc.scalar.activation(
+                    out=x_unread[:, 1, j, :], in_=x_sb[b][:, 1, j * POS : (j + 1) * POS], func=ACT.Square,
+                    bias=x_neg_mean[:, j : j + 1], accum_out=x_sum_sq[b][:, j : j + 1],
+                )
 
         def quantise_image(b):
             std = small.tile([P, ROWS], F32)
-            nc.scalar.activation(out=std[:], in_=mean_var[b][:, :, 1], func=ACT.Sqrt, scale=POS / (POS - 1.0))
+            nc.scalar.activation(out=std[:, 0:PACK], in_=mean_var[b][:, :, 1], func=ACT.Sqrt, scale=POS / (POS - 1.0))
+            nc.scalar.activation(out=std[:, PACK:ROWS], in_=x_sum_sq[b][:], func=ACT.Sqrt, scale=1.0 / (POS - 1.0))
             padded = small.tile([P, ROWS], F32)
             nc.vector.tensor_scalar_add(out=padded[:], in0=std[:], scalar1=1e-8)
             recip = small.tile([P, ROWS], F32)
@@ -205,9 +219,13 @@ def tile_axialattentionblock_pa_kernel(
             tiles["ln_std", n] = ln_std
             tiles["centred", n] = centred
 
-        def finish(n):
+        def invert(n):
             rstd = small.tile([P, QK, POS_TILES], F32)
             nc.vector.reciprocal(out=rstd[:], in_=tiles["ln_std", n][:])
+            tiles["rstd", n] = rstd
+
+        def finish(n):
+            rstd = tiles["rstd", n]
             qk_out = work.tile([P, QK, POS_TILES, HEAD], F32)
             for s, t in GROUPS:
                 nc.vector.scalar_tensor_tensor(
@@ -217,7 +235,12 @@ def tile_axialattentionblock_pa_kernel(
             for s, out in enumerate((out_0, out_1)):
                 nc.sync.dma_start(out=dram_head(out, n), in_=qk_out[:, s].rearrange("p t c -> p (t c)"))
 
-        image_statistics(0)
+        statistics_on_vector(0)
+        statistics_on_scalar(0)
+        statistics_on_vector(1)
+        quantise_image(0)
+        statistics_on_scalar(1)
+        quantise_image(1)
         neg_bias_mean = keep.tile([P, HEADS, QK], F32)
         bias_unread = keep.tile([P, HEADS, QK, HEAD], BF16)
         for h in range(HEADS):
@@ -226,16 +249,14 @@ def tile_axialattentionblock_pa_kernel(
                     out=bias_unread[:, h, s, :], in_=bias[:, h, s, :], func=ACT.Identity,
                     scale=-1.0 / HEAD, accum_out=neg_bias_mean[:, h, s : s + 1],
                 )
-        quantise_image(0)
         project(0)
-        image_statistics(1)
         for step in range(UNITS + 3):
-            if step == QUANTISE_STEP:
-                quantise_image(1)
             if step + 1 < UNITS:
                 project(step + 1)
             if step < UNITS:
                 leave_psum(step)
+            if step >= 3:
+                invert(step - 3)
             if 0 <= step - 2 < UNITS:
                 centre(step - 2)
             if step >= 3:

@@ -171,30 +171,26 @@ def tile_axialattentionblock_pa_kernel(
 
         def leave_psum(n):
             h = n % HEADS
-            v_out = work.tile([P, POS_TILES, HEAD], F32)
-            nc.vector.tensor_tensor(
-                out=v_out[:], in0=tiles["v_bank", n][:],
-                in1=bias[:, h, 2, :].unsqueeze(1).to_broadcast([P, POS_TILES, HEAD]), op=ALU.add,
-            )
-            nc.sync.dma_start(out=dram_head(out_2, n), in_=v_out[:].rearrange("p t c -> p (t c)"))
-            y = work.tile([P, QK, POS_TILES, HEAD], F32)
+            y = work.tile([P, 3, POS_TILES, HEAD], F32)
             sum_y = small.tile([P, QK, POS_TILES], F32)
             for s, t in GROUPS:
                 nc.scalar.activation(
                     out=y[:, s, t, :], in_=tiles["qk_bank%d" % (t // 2), n][:, t % 2, s, :], func=ACT.Identity,
                     accum_out=sum_y[:, s, t : t + 1],
                 )
+            nc.scalar.copy(out=y[:, 2], in_=tiles["v_bank", n][:])
             neg_mean = small.tile([P, QK, POS_TILES], F32)
             for s in range(QK):
-                nc.gpsimd.tensor_scalar(
-                    out=neg_mean[:, s, :], in0=sum_y[:, s, :], scalar1=-1.0 / HEAD,
-                    scalar2=neg_bias_mean[:, h, s : s + 1], op0=ALU.mult, op1=ALU.add,
+                nc.scalar.activation(
+                    out=neg_mean[:, s, :], in_=sum_y[:, s, :], func=ACT.Identity,
+                    scale=-1.0 / HEAD, bias=neg_bias_mean[:, h, s : s + 1],
                 )
-            u = work.tile([P, QK, POS_TILES, HEAD], F32, bufs=5)
+            u = work.tile([P, 3, POS_TILES, HEAD], F32, bufs=5)
             nc.gpsimd.tensor_tensor(
                 out=u[:], in0=y[:],
-                in1=bias[:, h, 0:QK, :].unsqueeze(2).to_broadcast([P, QK, POS_TILES, HEAD]), op=ALU.add,
+                in1=bias[:, h].unsqueeze(2).to_broadcast([P, 3, POS_TILES, HEAD]), op=ALU.add,
             )
+            nc.sync.dma_start(out=dram_head(out_2, n), in_=u[:, 2].rearrange("p t c -> p (t c)"))
             tiles["u", n] = u
             tiles["neg_mean", n] = neg_mean
 

@@ -41,11 +41,22 @@ def tile_axialattentionblock_pa_kernel(
         const_psum = stack.enter_context(tc.psum_pool(name="const_psum", bufs=1))
         stack.enter_context(tc.manual_schedule())
 
+        ln_eps = keep.tile([P, 1], F32)
+        nc.vector.memset(ln_eps[:], 1e-5)
+        warm = keep.tile([P, 1], F32)
+        nc.scalar.activation(out=warm[:], in_=ln_eps[:], func=ACT.Sqrt)
+
         x_rows = x.rearrange("b (g p j) h w -> b g p (j h w)", g=PASSES, p=P, j=PACK)
         x_sb = [keep.tile([P, PASSES, PACK * POS], BF16, name="x_sb%d" % b) for b in range(BATCH)]
+        w1 = keep.tile([P, ROWS], BF16)
         for b in range(BATCH):
             for g in range(PASSES):
                 nc.sync.dma_start(out=x_sb[b][:, g, :], in_=x_rows[b, g])
+            if b == 0:
+                nc.sync.dma_start(
+                    out=w1[:].rearrange("p (g j) -> p g j", g=PASSES),
+                    in_=norm1_w.rearrange("(g p j) -> p g j", g=PASSES, p=P, j=PACK),
+                )
 
         w_planes = keep.tile([P, PASSES, OUT], U8, align_bytes=64)
         nc.vector.memset(w_planes[:].bitcast(I32), 0)
@@ -58,20 +69,18 @@ def tile_axialattentionblock_pa_kernel(
 
         w_words = keep.tile([P, PASSES, OUT], U32, align_bytes=64)
         words_dram = qkv_w_words.rearrange("g p n t -> p g (n t)")
+        bias = keep.tile([P, HEADS, 3, HEAD], BF16)
         chunk = 2 * 3 * HEAD
         for c0 in range(0, OUT, chunk):
+            nc.sync.dma_start(
+                out=bias[:].rearrange("p n s c -> p (n s c)")[:, c0 : c0 + chunk],
+                in_=qkv_b[c0 : c0 + chunk].partition_broadcast(P),
+            )
             nc.sync.dma_start(
                 out=w_words[:, :, c0 : c0 + chunk].bitcast(I32),
                 in_=words_dram[:, :, PACK * c0 : PACK * (c0 + chunk)].bitcast(I32),
             )
 
-        w1 = keep.tile([P, ROWS], BF16)
-        nc.scalar.dma_start(
-            out=w1[:].rearrange("p (g j) -> p g j", g=PASSES),
-            in_=norm1_w.rearrange("(g p j) -> p g j", g=PASSES, p=P, j=PACK),
-        )
-        bias = keep.tile([P, HEADS, 3, HEAD], BF16)
-        nc.scalar.dma_start(out=bias[:].rearrange("p n s c -> p (n s c)"), in_=qkv_b.partition_broadcast(P))
         ln_rows = keep.tile([P, 2, QK, HEAD], BF16)
         nc.vector.memset(ln_rows[:], 0.0)
         for s, (w_vec, b_vec) in enumerate(((qn_w, qn_b), (kn_w, kn_b))):
@@ -79,8 +88,6 @@ def tile_axialattentionblock_pa_kernel(
             nc.scalar.dma_start(out=ln_rows[0:1, 1, s, :], in_=b_vec.unsqueeze(0))
         ones = keep.tile([P, P], BF16)
         nc.vector.memset(ones[:], 1.0)
-        ln_eps = keep.tile([P, 1], F32)
-        nc.vector.memset(ln_eps[:], 1e-5)
         ln_bank = const_psum.tile([P, 2, QK, HEAD], F32)
         nc.tensor.matmul(
             out=ln_bank[:].rearrange("p a s c -> p (a s c)"), lhsT=ones[:],
@@ -171,26 +178,30 @@ def tile_axialattentionblock_pa_kernel(
 
         def leave_psum(n):
             h = n % HEADS
-            y = work.tile([P, 3, POS_TILES, HEAD], F32)
+            v_out = work.tile([P, POS_TILES, HEAD], F32)
+            nc.vector.tensor_tensor(
+                out=v_out[:], in0=tiles["v_bank", n][:],
+                in1=bias[:, h, 2, :].unsqueeze(1).to_broadcast([P, POS_TILES, HEAD]), op=ALU.add,
+            )
+            nc.sync.dma_start(out=dram_head(out_2, n), in_=v_out[:].rearrange("p t c -> p (t c)"))
+            y = work.tile([P, QK, POS_TILES, HEAD], F32)
             sum_y = small.tile([P, QK, POS_TILES], F32)
             for s, t in GROUPS:
                 nc.scalar.activation(
                     out=y[:, s, t, :], in_=tiles["qk_bank%d" % (t // 2), n][:, t % 2, s, :], func=ACT.Identity,
                     accum_out=sum_y[:, s, t : t + 1],
                 )
-            nc.scalar.copy(out=y[:, 2], in_=tiles["v_bank", n][:])
             neg_mean = small.tile([P, QK, POS_TILES], F32)
             for s in range(QK):
-                nc.scalar.activation(
-                    out=neg_mean[:, s, :], in_=sum_y[:, s, :], func=ACT.Identity,
-                    scale=-1.0 / HEAD, bias=neg_bias_mean[:, h, s : s + 1],
+                nc.gpsimd.tensor_scalar(
+                    out=neg_mean[:, s, :], in0=sum_y[:, s, :], scalar1=-1.0 / HEAD,
+                    scalar2=neg_bias_mean[:, h, s : s + 1], op0=ALU.mult, op1=ALU.add,
                 )
-            u = work.tile([P, 3, POS_TILES, HEAD], F32, bufs=5)
+            u = work.tile([P, QK, POS_TILES, HEAD], F32, bufs=5)
             nc.gpsimd.tensor_tensor(
                 out=u[:], in0=y[:],
-                in1=bias[:, h].unsqueeze(2).to_broadcast([P, 3, POS_TILES, HEAD]), op=ALU.add,
+                in1=bias[:, h, 0:QK, :].unsqueeze(2).to_broadcast([P, QK, POS_TILES, HEAD]), op=ALU.add,
             )
-            nc.sync.dma_start(out=dram_head(out_2, n), in_=u[:, 2].rearrange("p t c -> p (t c)"))
             tiles["u", n] = u
             tiles["neg_mean", n] = neg_mean
 

@@ -24,6 +24,14 @@ ROWS = PASSES * PACK
 QK = 2
 GROUPS = [(s, t) for s in range(QK) for t in range(POS_TILES)]
 UNITS = BATCH * HEADS
+LOAD_COLUMNS = 2 * 3 * HEAD
+
+STAGE_BUFS = 2
+SMALL_BUFS = 6
+WORK_BUFS = 3
+U_BUFS = 5
+BANK_BUFS = 2
+V_BANK_BUFS = 3
 
 FLOPS = 2 * BATCH * POS * (PASSES * P * PACK) * OUT
 
@@ -34,10 +42,10 @@ def tile_axialattentionblock_pa_kernel(
     nc = tc.nc
     with ExitStack() as stack:
         keep = stack.enter_context(tc.tile_pool(name="keep", bufs=1))
-        stage = stack.enter_context(tc.tile_pool(name="stage", bufs=2))
-        small = stack.enter_context(tc.tile_pool(name="small", bufs=6))
-        work = stack.enter_context(tc.tile_pool(name="work", bufs=3))
-        psum = stack.enter_context(tc.psum_pool(name="psum", bufs=2))
+        stage = stack.enter_context(tc.tile_pool(name="stage", bufs=STAGE_BUFS))
+        small = stack.enter_context(tc.tile_pool(name="small", bufs=SMALL_BUFS))
+        work = stack.enter_context(tc.tile_pool(name="work", bufs=WORK_BUFS))
+        psum = stack.enter_context(tc.psum_pool(name="psum", bufs=BANK_BUFS))
         const_psum = stack.enter_context(tc.psum_pool(name="const_psum", bufs=1))
         stack.enter_context(tc.manual_schedule())
 
@@ -46,12 +54,12 @@ def tile_axialattentionblock_pa_kernel(
         warm = keep.tile([P, 1], F32)
         nc.scalar.activation(out=warm[:], in_=ln_eps[:], func=ACT.Sqrt)
 
-        x_rows = x.rearrange("b (g p j) h w -> b g p (j h w)", g=PASSES, p=P, j=PACK)
+        x_dram = x.rearrange("b (g p j) hh ww -> b g p (j hh ww)", g=PASSES, p=P, j=PACK)
         x_sb = [keep.tile([P, PASSES, PACK * POS], BF16, name="x_sb%d" % b) for b in range(BATCH)]
         w1 = keep.tile([P, ROWS], BF16)
         for b in range(BATCH):
             for g in range(PASSES):
-                nc.sync.dma_start(out=x_sb[b][:, g, :], in_=x_rows[b, g])
+                nc.sync.dma_start(out=x_sb[b][:, g, :], in_=x_dram[b, g])
             if b == 0:
                 nc.sync.dma_start(
                     out=w1[:].rearrange("p (g j) -> p g j", g=PASSES),
@@ -60,25 +68,24 @@ def tile_axialattentionblock_pa_kernel(
 
         w_planes = keep.tile([P, PASSES, OUT], U8, align_bytes=64)
         nc.vector.memset(w_planes[:].bitcast(I32), 0)
-        scale_rows = qkv_w_scales.rearrange("g (i a r) n -> a r i g n", i=2, a=2, r=4)
-        for a in range(2):
+        scales_dram = qkv_w_scales.rearrange("g (i odd r) o -> odd r i g o", i=2, odd=2, r=4)
+        for odd in range(2):
             for r in range(4):
                 nc.sync.dma_start(
-                    out=w_planes[32 * a + r : P : 64].bitcast(I32), in_=scale_rows[a, r].bitcast(I32)
+                    out=w_planes[32 * odd + r : P : 64].bitcast(I32), in_=scales_dram[odd, r].bitcast(I32)
                 )
 
         w_words = keep.tile([P, PASSES, OUT], U32, align_bytes=64)
-        words_dram = qkv_w_words.rearrange("g p n t -> p g (n t)")
+        words_dram = qkv_w_words.rearrange("g p o e -> p g (o e)")
         bias = keep.tile([P, HEADS, 3, HEAD], BF16)
-        chunk = 2 * 3 * HEAD
-        for c0 in range(0, OUT, chunk):
+        for c0 in range(0, OUT, LOAD_COLUMNS):
             nc.sync.dma_start(
-                out=bias[:].rearrange("p n s c -> p (n s c)")[:, c0 : c0 + chunk],
-                in_=qkv_b[c0 : c0 + chunk].partition_broadcast(P),
+                out=bias[:].rearrange("p h s c -> p (h s c)")[:, c0 : c0 + LOAD_COLUMNS],
+                in_=qkv_b[c0 : c0 + LOAD_COLUMNS].partition_broadcast(P),
             )
             nc.sync.dma_start(
-                out=w_words[:, :, c0 : c0 + chunk].bitcast(I32),
-                in_=words_dram[:, :, PACK * c0 : PACK * (c0 + chunk)].bitcast(I32),
+                out=w_words[:, :, c0 : c0 + LOAD_COLUMNS].bitcast(I32),
+                in_=words_dram[:, :, PACK * c0 : PACK * (c0 + LOAD_COLUMNS)].bitcast(I32),
             )
 
         ln_rows = keep.tile([P, 2, QK, HEAD], BF16)
@@ -90,8 +97,8 @@ def tile_axialattentionblock_pa_kernel(
         nc.vector.memset(ones[:], 1.0)
         ln_bank = const_psum.tile([P, 2, QK, HEAD], F32)
         nc.tensor.matmul(
-            out=ln_bank[:].rearrange("p a s c -> p (a s c)"), lhsT=ones[:],
-            rhs=ln_rows[:].rearrange("p a s c -> p (a s c)"), start=True, stop=True,
+            out=ln_bank[:].rearrange("p v s c -> p (v s c)"), lhsT=ones[:],
+            rhs=ln_rows[:].rearrange("p v s c -> p (v s c)"), start=True, stop=True,
         )
         gain = ln_bank[:, 0]
         shift = ln_bank[:, 1]
@@ -149,18 +156,18 @@ def tile_axialattentionblock_pa_kernel(
                 )
 
         def dram_head(out, n):
-            return out.rearrange("b n y x c -> (b n) (y x c)")[n].rearrange("(m f) -> m f", m=P)
+            return out.rearrange("b h hh ww c -> (b h) (hh ww c)")[n].rearrange("(m f) -> m f", m=P)
 
         tiles = {}
 
         def project(n):
             b, h = divmod(n, HEADS)
             c0 = h * 3 * HEAD
-            for a in range(2):
-                tiles["qk_bank%d" % a, n] = psum.tile([P, 2, QK, HEAD], F32, name="qk_bank%d" % a)
-            tiles["v_bank", n] = psum.tile([P, POS_TILES, HEAD], F32, name="v_bank", bufs=3)
+            for pair in range(2):
+                tiles["qk_bank%d" % pair, n] = psum.tile([P, 2, QK, HEAD], F32, name="qk_bank%d" % pair)
+            tiles["v_bank", n] = psum.tile([P, POS_TILES, HEAD], F32, name="v_bank", bufs=V_BANK_BUFS)
             for t in range(POS_TILES):
-                rows = slice(t * P, (t + 1) * P)
+                positions = slice(t * P, (t + 1) * P)
                 for acc, cols in (
                     (tiles["qk_bank%d" % (t // 2), n][:, t % 2].rearrange("p s c -> p (s c)"), slice(c0, c0 + QK * HEAD)),
                     (tiles["v_bank", n][:, t, :], slice(c0 + QK * HEAD, c0 + 3 * HEAD)),
@@ -168,8 +175,8 @@ def tile_axialattentionblock_pa_kernel(
                     for g in range(PASSES):
                         nc.tensor.matmul_mx(
                             out=acc,
-                            lhsT=h_codes[b][:, g, rows].bitcast(FP8X4),
-                            lhsT_scale=h_planes[b][:, g, rows],
+                            lhsT=h_codes[b][:, g, positions].bitcast(FP8X4),
+                            lhsT_scale=h_planes[b][:, g, positions],
                             rhs=w_words[:, g, cols].bitcast(FP8X4),
                             rhs_scale=w_planes[:, g, cols],
                             start=(g == 0),
@@ -188,7 +195,7 @@ def tile_axialattentionblock_pa_kernel(
             sum_y = small.tile([P, QK, POS_TILES], F32)
             for s, t in GROUPS:
                 nc.scalar.activation(
-                    out=y[:, s, t, :], in_=tiles["qk_bank%d" % (t // 2), n][:, t % 2, s, :], func=ACT.Identity,
+                    out=y[:, s, t, :], in_=tiles["qk_bank%d" % (t // 2), n][:, t % 2, s, :], func=ACT.Copy,
                     accum_out=sum_y[:, s, t : t + 1],
                 )
             neg_mean = small.tile([P, QK, POS_TILES], F32)
@@ -197,7 +204,7 @@ def tile_axialattentionblock_pa_kernel(
                     out=neg_mean[:, s, :], in0=sum_y[:, s, :], scalar1=-1.0 / HEAD,
                     scalar2=neg_bias_mean[:, h, s : s + 1], op0=ALU.mult, op1=ALU.add,
                 )
-            u = work.tile([P, QK, POS_TILES, HEAD], F32, bufs=5)
+            u = work.tile([P, QK, POS_TILES, HEAD], F32, bufs=U_BUFS)
             nc.gpsimd.tensor_tensor(
                 out=u[:], in0=y[:],
                 in1=bias[:, h, 0:QK, :].unsqueeze(2).to_broadcast([P, QK, POS_TILES, HEAD]), op=ALU.add,
@@ -205,25 +212,30 @@ def tile_axialattentionblock_pa_kernel(
             tiles["u", n] = u
             tiles["neg_mean", n] = neg_mean
 
-        def centre(n):
-            u = tiles["u", n]
-            neg_mean = tiles["neg_mean", n]
+        def sum_squares(n):
             unread = work.tile([P, QK, POS_TILES, HEAD], BF16)
             sum_sq = small.tile([P, QK, POS_TILES], F32)
             for s, t in GROUPS:
                 nc.scalar.activation(
-                    out=unread[:, s, t, :], in_=u[:, s, t, :], func=ACT.Square,
-                    bias=neg_mean[:, s, t : t + 1], accum_out=sum_sq[:, s, t : t + 1],
+                    out=unread[:, s, t, :], in_=tiles["u", n][:, s, t, :], func=ACT.Square,
+                    bias=tiles["neg_mean", n][:, s, t : t + 1], accum_out=sum_sq[:, s, t : t + 1],
                 )
+            tiles["sum_sq", n] = sum_sq
+
+        def take_root(n):
             ln_std = small.tile([P, QK, POS_TILES], F32)
-            nc.scalar.activation(out=ln_std[:], in_=sum_sq[:], func=ACT.Sqrt, scale=1.0 / HEAD, bias=ln_eps[:, 0:1])
+            nc.scalar.activation(
+                out=ln_std[:], in_=tiles["sum_sq", n][:], func=ACT.Sqrt, scale=1.0 / HEAD, bias=ln_eps[:, 0:1]
+            )
+            tiles["ln_std", n] = ln_std
+
+        def centre(n):
             centred = work.tile([P, QK, POS_TILES, HEAD], F32)
             for s, t in GROUPS:
                 nc.vector.scalar_tensor_tensor(
-                    out=centred[:, s, t, :], in0=u[:, s, t, :], scalar=neg_mean[:, s, t : t + 1],
+                    out=centred[:, s, t, :], in0=tiles["u", n][:, s, t, :], scalar=tiles["neg_mean", n][:, s, t : t + 1],
                     in1=gain[:, s, :], op0=ALU.add, op1=ALU.mult,
                 )
-            tiles["ln_std", n] = ln_std
             tiles["centred", n] = centred
 
         def invert(n):
@@ -260,8 +272,12 @@ def tile_axialattentionblock_pa_kernel(
         for step in range(UNITS + 3):
             if step + 1 < UNITS:
                 project(step + 1)
+            if 0 <= step - 2 < UNITS:
+                sum_squares(step - 2)
             if step < UNITS:
                 leave_psum(step)
+            if 0 <= step - 2 < UNITS:
+                take_root(step - 2)
             if step >= 3:
                 invert(step - 3)
             if 0 <= step - 2 < UNITS:

@@ -143,9 +143,9 @@ def tile_axialattentionblock_pa_kernel(
             for g in range(PASSES):
                 grouped.append(stage.tile([P, POS, PACK], BF16, name="grouped%d" % g, align_bytes=64))
                 nc.vector.tensor_tensor(
-                    out=grouped[g][:].rearrange("p (t m) j -> p t m j", t=POS_TILES),
-                    in0=x_sb[b][:, g, :].rearrange("p (j m t) -> p t m j", j=PACK, t=POS_TILES),
-                    in1=factor[:, g * PACK : (g + 1) * PACK].unsqueeze(1).unsqueeze(1).to_broadcast([P, POS_TILES, P, PACK]),
+                    out=grouped[g][:].rearrange("p (t m) j -> p m j t", t=POS_TILES),
+                    in0=x_sb[b][:, g, :].rearrange("p (j m t) -> p m j t", j=PACK, t=POS_TILES),
+                    in1=factor[:, g * PACK : (g + 1) * PACK].unsqueeze(1).unsqueeze(3).to_broadcast([P, P, PACK, POS_TILES]),
                     op=ALU.mult,
                 )
             for g in range(PASSES):

@@ -139,14 +139,19 @@ def tile_axialattentionblock_pa_kernel(
             nc.vector.reciprocal(out=recip[:], in_=padded[:])
             factor = small.tile([P, ROWS], F32)
             nc.vector.tensor_tensor(out=factor[:], in0=recip[:], in1=w1[:], op=ALU.mult)
+            scaled = stage.tile([P, PASSES, PACK * POS], BF16)
+            for g in range(PASSES):
+                for j in range(PACK):
+                    nc.vector.tensor_scalar_mul(
+                        out=scaled[:, g, j * POS : (j + 1) * POS], in0=x_sb[b][:, g, j * POS : (j + 1) * POS],
+                        scalar1=factor[:, g * PACK + j : g * PACK + j + 1],
+                    )
             grouped = []
             for g in range(PASSES):
                 grouped.append(stage.tile([P, POS, PACK], BF16, name="grouped%d" % g, align_bytes=64))
-                nc.vector.tensor_tensor(
+                nc.vector.tensor_copy(
                     out=grouped[g][:].rearrange("p (t m) j -> p m j t", t=POS_TILES),
-                    in0=x_sb[b][:, g, :].rearrange("p (j m t) -> p m j t", j=PACK, t=POS_TILES),
-                    in1=factor[:, g * PACK : (g + 1) * PACK].unsqueeze(1).unsqueeze(3).to_broadcast([P, P, PACK, POS_TILES]),
-                    op=ALU.mult,
+                    in_=scaled[:, g, :].rearrange("p (j m t) -> p m j t", j=PACK, t=POS_TILES),
                 )
             for g in range(PASSES):
                 nc.vector.quantize_mx(

@@ -1,6 +1,7 @@
 from contextlib import ExitStack
 
 import concourse.mybir as mybir
+from concourse.masks import make_identity
 
 F32 = mybir.dt.float32
 BF16 = mybir.dt.bfloat16
@@ -25,6 +26,8 @@ QK = 2
 GROUPS = [(s, t) for s in range(QK) for t in range(POS_TILES)]
 UNITS = BATCH * HEADS
 LOAD_COLUMNS = 2 * 3 * HEAD
+BIAS_GROUPS = OUT // HEAD
+VECTOR_ROWS = (6, 4)
 
 STAGE_BUFS = 2
 SMALL_BUFS = 6
@@ -95,6 +98,11 @@ def tile_axialattentionblock_pa_kernel(
             nc.scalar.dma_start(out=ln_rows[0:1, 1, s, :], in_=b_vec.unsqueeze(0))
         ones = keep.tile([P, P], BF16)
         nc.vector.memset(ones[:], 1.0)
+        bias_rows = keep.tile([P, HEAD], BF16)
+        nc.vector.memset(bias_rows[:], 0.0)
+        nc.scalar.dma_start(out=bias_rows[0:BIAS_GROUPS, :], in_=qkv_b.rearrange("(r c) -> r c", c=HEAD))
+        identity = keep.tile([P, P], F32)
+        make_identity(nc, identity[:])
         ln_bank = const_psum.tile([P, 2, QK, HEAD], F32)
         nc.tensor.matmul(
             out=ln_bank[:].rearrange("p v s c -> p (v s c)"), lhsT=ones[:],
@@ -105,34 +113,38 @@ def tile_axialattentionblock_pa_kernel(
 
         h_codes = [keep.tile([P, PASSES, POS], U32, name="h_codes%d" % b, align_bytes=64) for b in range(BATCH)]
         h_planes = [keep.tile([P, PASSES, POS], U8, name="h_planes%d" % b, align_bytes=64) for b in range(BATCH)]
-        mean_var = [keep.tile([P, PACK, 2], F32, name="mean_var%d" % b) for b in range(BATCH)]
-        x_sum_sq = [keep.tile([P, PACK], F32, name="x_sum_sq%d" % b) for b in range(BATCH)]
+        mean_var = [keep.tile([P, ROWS, 2], F32, name="mean_var%d" % b) for b in range(BATCH)]
+        x_sum_sq = [keep.tile([P, ROWS], F32, name="x_sum_sq%d" % b) for b in range(BATCH)]
+
+        def x_row(b, r):
+            return x_sb[b][:, r // PACK, (r % PACK) * POS : (r % PACK + 1) * POS]
 
         def statistics_on_vector(b):
-            stats = small.tile([P, PACK, 6], F32)
-            for j in range(PACK):
-                nc.vector.bn_stats(out=stats[:, j, :], in_=x_sb[b][:, 0, j * POS : (j + 1) * POS])
-            for j in range(PACK):
-                nc.vector.bn_aggr(out=mean_var[b][:, j, :], in_=stats[:, j, :])
+            stats = small.tile([P, ROWS, 6], F32)
+            for r in range(VECTOR_ROWS[b]):
+                nc.vector.bn_stats(out=stats[:, r, :], in_=x_row(b, r))
+            for r in range(VECTOR_ROWS[b]):
+                nc.vector.bn_aggr(out=mean_var[b][:, r, :], in_=stats[:, r, :])
 
         def statistics_on_scalar(b):
-            x_unread = stage.tile([P, 2, PACK, POS], BF16)
-            x_neg_mean = small.tile([P, PACK], F32)
-            for j in range(PACK):
+            x_unread = stage.tile([P, 2, ROWS, POS], BF16)
+            x_neg_mean = small.tile([P, ROWS], F32)
+            for r in range(VECTOR_ROWS[b], ROWS):
                 nc.scalar.activation(
-                    out=x_unread[:, 0, j, :], in_=x_sb[b][:, 1, j * POS : (j + 1) * POS], func=ACT.Identity,
-                    scale=-1.0 / POS, accum_out=x_neg_mean[:, j : j + 1],
+                    out=x_unread[:, 0, r, :], in_=x_row(b, r), func=ACT.Identity,
+                    scale=-1.0 / POS, accum_out=x_neg_mean[:, r : r + 1],
                 )
-            for j in range(PACK):
+            for r in range(VECTOR_ROWS[b], ROWS):
                 nc.scalar.activation(
-                    out=x_unread[:, 1, j, :], in_=x_sb[b][:, 1, j * POS : (j + 1) * POS], func=ACT.Square,
-                    bias=x_neg_mean[:, j : j + 1], accum_out=x_sum_sq[b][:, j : j + 1],
+                    out=x_unread[:, 1, r, :], in_=x_row(b, r), func=ACT.Square,
+                    bias=x_neg_mean[:, r : r + 1], accum_out=x_sum_sq[b][:, r : r + 1],
                 )
 
         def quantise_image(b):
             std = small.tile([P, ROWS], F32)
-            nc.scalar.activation(out=std[:, 0:PACK], in_=mean_var[b][:, :, 1], func=ACT.Sqrt, scale=POS / (POS - 1.0))
-            nc.scalar.activation(out=std[:, PACK:ROWS], in_=x_sum_sq[b][:], func=ACT.Sqrt, scale=1.0 / (POS - 1.0))
+            split = VECTOR_ROWS[b]
+            nc.scalar.activation(out=std[:, 0:split], in_=mean_var[b][:, 0:split, 1], func=ACT.Sqrt, scale=POS / (POS - 1.0))
+            nc.scalar.activation(out=std[:, split:ROWS], in_=x_sum_sq[b][:, split:ROWS], func=ACT.Sqrt, scale=1.0 / (POS - 1.0))
             padded = small.tile([P, ROWS], F32)
             nc.vector.tensor_scalar_add(out=padded[:], in0=std[:], scalar1=1e-8)
             recip = small.tile([P, ROWS], F32)
@@ -261,20 +273,22 @@ def tile_axialattentionblock_pa_kernel(
 
         statistics_on_vector(0)
         statistics_on_scalar(0)
-        statistics_on_vector(1)
         quantise_image(0)
+        bias_unread = keep.tile([P, HEAD], BF16)
+        neg_mean_column = keep.tile([P, 1], F32)
+        nc.scalar.activation(
+            out=bias_unread[:], in_=bias_rows[:], func=ACT.Identity, scale=-1.0 / HEAD, accum_out=neg_mean_column[:],
+        )
+        spread = psum.tile([P, POS_TILES, HEAD], F32, name="v_bank", bufs=V_BANK_BUFS)
+        nc.tensor.matmul(
+            out=spread[:, 0, :], lhsT=neg_mean_column[:, 0:1].to_broadcast([P, P]), rhs=identity[:], start=True, stop=True,
+        )
+        neg_bias_mean = keep.tile([P, HEADS, 3], F32)
+        nc.vector.tensor_copy(out=neg_bias_mean[:].rearrange("p h s -> p (h s)"), in_=spread[:, 0, 0:BIAS_GROUPS])
+        statistics_on_vector(1)
         statistics_on_scalar(1)
-        quantise_image(1)
-        neg_bias_mean = keep.tile([P, HEADS, QK], F32)
-        bias_unread = keep.tile([P, HEADS, QK, HEAD], BF16)
-        for h in range(HEADS):
-            for s in range(QK):
-                nc.scalar.activation(
-                    out=bias_unread[:, h, s, :], in_=bias[:, h, s, :], func=ACT.Identity,
-                    scale=-1.0 / HEAD, accum_out=neg_bias_mean[:, h, s : s + 1],
-                )
         project(0)
-        for step in range(UNITS + 3):
+        def pipeline_step(step):
             if step + 1 < UNITS:
                 project(step + 1)
             if 0 <= step - 2 < UNITS:
@@ -289,3 +303,8 @@ def tile_axialattentionblock_pa_kernel(
                 centre(step - 2)
             if step >= 3:
                 finish(step - 3)
+
+        pipeline_step(0)
+        quantise_image(1)
+        for step in range(1, UNITS + 3):
+            pipeline_step(step)

@@ -83,12 +83,12 @@ def tile_axialattentionblock_pa_kernel(
         bias = keep.tile([P, HEADS, 3, HEAD], BF16)
         for c0 in range(0, OUT, LOAD_COLUMNS):
             nc.sync.dma_start(
-                out=bias[:].rearrange("p h s c -> p (h s c)")[:, c0 : c0 + LOAD_COLUMNS],
-                in_=qkv_b[c0 : c0 + LOAD_COLUMNS].partition_broadcast(P),
-            )
-            nc.sync.dma_start(
                 out=w_words[:, :, c0 : c0 + LOAD_COLUMNS].bitcast(I32),
                 in_=words_dram[:, :, PACK * c0 : PACK * (c0 + LOAD_COLUMNS)].bitcast(I32),
+            )
+            nc.sync.dma_start(
+                out=bias[:].rearrange("p h s c -> p (h s c)")[:, c0 : c0 + LOAD_COLUMNS],
+                in_=qkv_b[c0 : c0 + LOAD_COLUMNS].partition_broadcast(P),
             )
 
         ln_rows = keep.tile([P, 2, QK, HEAD], BF16)

@@ -27,6 +27,7 @@ GROUPS = [(s, t) for s in range(QK) for t in range(POS_TILES)]
 UNITS = BATCH * HEADS
 LOAD_COLUMNS = 2 * 3 * HEAD
 BIAS_GROUPS = OUT // HEAD
+BIAS_BANKS = 3
 VECTOR_ROWS = (6, 4)
 
 STAGE_BUFS = 2
@@ -80,15 +81,10 @@ def tile_axialattentionblock_pa_kernel(
 
         w_words = keep.tile([P, PASSES, OUT], U32, align_bytes=64)
         words_dram = qkv_w_words.rearrange("g p o e -> p g (o e)")
-        bias = keep.tile([P, HEADS, 3, HEAD], BF16)
         for c0 in range(0, OUT, LOAD_COLUMNS):
             nc.sync.dma_start(
                 out=w_words[:, :, c0 : c0 + LOAD_COLUMNS].bitcast(I32),
                 in_=words_dram[:, :, PACK * c0 : PACK * (c0 + LOAD_COLUMNS)].bitcast(I32),
-            )
-            nc.sync.dma_start(
-                out=bias[:].rearrange("p h s c -> p (h s c)")[:, c0 : c0 + LOAD_COLUMNS],
-                in_=qkv_b[c0 : c0 + LOAD_COLUMNS].partition_broadcast(P),
             )
 
         ln_rows = keep.tile([P, 2, QK, HEAD], BF16)
@@ -108,6 +104,19 @@ def tile_axialattentionblock_pa_kernel(
             out=ln_bank[:].rearrange("p v s c -> p (v s c)"), lhsT=ones[:],
             rhs=ln_rows[:].rearrange("p v s c -> p (v s c)"), start=True, stop=True,
         )
+        identity_bf16 = keep.tile([P, P], BF16)
+        make_identity(nc, identity_bf16[:])
+        bias = keep.tile([P, HEADS, 3, HEAD], BF16)
+        bias_banks = []
+        for i in range(BIAS_BANKS):
+            bias_bank = psum.tile([P, BIAS_GROUPS // BIAS_BANKS, HEAD], BF16, name="v_bank", bufs=V_BANK_BUFS)
+            for r in range(BIAS_GROUPS // BIAS_BANKS):
+                row = i * (BIAS_GROUPS // BIAS_BANKS) + r
+                nc.tensor.matmul(
+                    out=bias_bank[:, r, :], lhsT=identity_bf16[:, row : row + 1].to_broadcast([P, P]),
+                    rhs=bias_rows[:], start=True, stop=True,
+                )
+            bias_banks.append(bias_bank)
         gain = ln_bank[:, 0]
         shift = ln_bank[:, 1]
 
@@ -279,6 +288,10 @@ def tile_axialattentionblock_pa_kernel(
         nc.scalar.activation(
             out=bias_unread[:], in_=bias_rows[:], func=ACT.Identity, scale=-1.0 / HEAD, accum_out=neg_mean_column[:],
         )
+        for i, bias_bank in enumerate(bias_banks):
+            nc.scalar.copy(
+                out=bias[:].rearrange("p h s c -> p (h s) c")[:, 8 * i : 8 * (i + 1), :], in_=bias_bank[:]
+            )
         spread = psum.tile([P, POS_TILES, HEAD], F32, name="v_bank", bufs=V_BANK_BUFS)
         nc.tensor.matmul(
             out=spread[:, 0, :], lhsT=neg_mean_column[:, 0:1].to_broadcast([P, P]), rhs=identity[:], start=True, stop=True,

@@ -28,7 +28,9 @@ UNITS = BATCH * HEADS
 LOAD_COLUMNS = 2 * 3 * HEAD
 BIAS_GROUPS = OUT // HEAD
 BIAS_BANKS = 3
-VECTOR_ROWS = (6, 4)
+BIAS_STEPS = {1: 1, 3: 2}
+SCALAR_ROWS = (2, 4)
+IMAGE_0_PIECES = ((2, 1), (3, 1), (0, 2), (4, 2), (6, 2))
 
 STAGE_BUFS = 2
 SMALL_BUFS = 6
@@ -58,17 +60,28 @@ def tile_axialattentionblock_pa_kernel(
         warm = keep.tile([P, 1], F32)
         nc.scalar.activation(out=warm[:], in_=ln_eps[:], func=ACT.Sqrt)
 
+        ln_rows = keep.tile([P, 2, QK, HEAD], BF16)
+        nc.vector.memset(ln_rows[:], 0.0)
+        ones = keep.tile([P, P], BF16)
+        nc.vector.memset(ones[:], 1.0)
+        bias_rows = keep.tile([P, HEAD], BF16)
+        nc.vector.memset(bias_rows[:], 0.0)
         x_dram = x.rearrange("b (g p j) hh ww -> b g p (j hh ww)", g=PASSES, p=P, j=PACK)
         x_sb = [keep.tile([P, PASSES, PACK * POS], BF16, name="x_sb%d" % b) for b in range(BATCH)]
         w1 = keep.tile([P, ROWS], BF16)
         for b in range(BATCH):
-            for g in range(PASSES):
-                nc.sync.dma_start(out=x_sb[b][:, g, :], in_=x_dram[b, g])
+            for r, count in IMAGE_0_PIECES if b == 0 else ((0, PACK), (PACK, PACK)):
+                columns = slice((r % PACK) * POS, (r % PACK + count) * POS)
+                nc.sync.dma_start(out=x_sb[b][:, r // PACK, columns], in_=x_dram[b, r // PACK][:, columns])
             if b == 0:
                 nc.sync.dma_start(
                     out=w1[:].rearrange("p (g j) -> p g j", g=PASSES),
                     in_=norm1_w.rearrange("(g p j) -> p g j", g=PASSES, p=P, j=PACK),
                 )
+                nc.sync.dma_start(out=bias_rows[0:BIAS_GROUPS, :], in_=qkv_b.rearrange("(r c) -> r c", c=HEAD))
+                for s, (w_vec, b_vec) in enumerate(((qn_w, qn_b), (kn_w, kn_b))):
+                    nc.sync.dma_start(out=ln_rows[0:1, 0, s, :], in_=w_vec.unsqueeze(0))
+                    nc.sync.dma_start(out=ln_rows[0:1, 1, s, :], in_=b_vec.unsqueeze(0))
 
         w_planes = keep.tile([P, PASSES, OUT], U8, align_bytes=64)
         nc.vector.memset(w_planes[:].bitcast(I32), 0)
@@ -87,16 +100,6 @@ def tile_axialattentionblock_pa_kernel(
                 in_=words_dram[:, :, PACK * c0 : PACK * (c0 + LOAD_COLUMNS)].bitcast(I32),
             )
 
-        ln_rows = keep.tile([P, 2, QK, HEAD], BF16)
-        nc.vector.memset(ln_rows[:], 0.0)
-        for s, (w_vec, b_vec) in enumerate(((qn_w, qn_b), (kn_w, kn_b))):
-            nc.scalar.dma_start(out=ln_rows[0:1, 0, s, :], in_=w_vec.unsqueeze(0))
-            nc.scalar.dma_start(out=ln_rows[0:1, 1, s, :], in_=b_vec.unsqueeze(0))
-        ones = keep.tile([P, P], BF16)
-        nc.vector.memset(ones[:], 1.0)
-        bias_rows = keep.tile([P, HEAD], BF16)
-        nc.vector.memset(bias_rows[:], 0.0)
-        nc.scalar.dma_start(out=bias_rows[0:BIAS_GROUPS, :], in_=qkv_b.rearrange("(r c) -> r c", c=HEAD))
         identity = keep.tile([P, P], F32)
         make_identity(nc, identity[:])
         ln_bank = const_psum.tile([P, 2, QK, HEAD], F32)
@@ -107,8 +110,9 @@ def tile_axialattentionblock_pa_kernel(
         identity_bf16 = keep.tile([P, P], BF16)
         make_identity(nc, identity_bf16[:])
         bias = keep.tile([P, HEADS, 3, HEAD], BF16)
-        bias_banks = []
-        for i in range(BIAS_BANKS):
+        bias_banks = {}
+
+        def spread_bias_bank(i):
             bias_bank = psum.tile([P, BIAS_GROUPS // BIAS_BANKS, HEAD], BF16, name="v_bank", bufs=V_BANK_BUFS)
             for r in range(BIAS_GROUPS // BIAS_BANKS):
                 row = i * (BIAS_GROUPS // BIAS_BANKS) + r
@@ -116,7 +120,14 @@ def tile_axialattentionblock_pa_kernel(
                     out=bias_bank[:, r, :], lhsT=identity_bf16[:, row : row + 1].to_broadcast([P, P]),
                     rhs=bias_rows[:], start=True, stop=True,
                 )
-            bias_banks.append(bias_bank)
+            bias_banks[i] = bias_bank
+
+        def copy_bias_bank(i):
+            nc.scalar.copy(
+                out=bias[:].rearrange("p h s c -> p (h s) c")[:, 8 * i : 8 * (i + 1), :], in_=bias_banks[i][:]
+            )
+
+        spread_bias_bank(0)
         gain = ln_bank[:, 0]
         shift = ln_bank[:, 1]
 
@@ -130,20 +141,20 @@ def tile_axialattentionblock_pa_kernel(
 
         def statistics_on_vector(b):
             stats = small.tile([P, ROWS, 6], F32)
-            for r in range(VECTOR_ROWS[b]):
+            for r in range(SCALAR_ROWS[b], ROWS):
                 nc.vector.bn_stats(out=stats[:, r, :], in_=x_row(b, r))
-            for r in range(VECTOR_ROWS[b]):
+            for r in range(SCALAR_ROWS[b], ROWS):
                 nc.vector.bn_aggr(out=mean_var[b][:, r, :], in_=stats[:, r, :])
 
         def statistics_on_scalar(b):
             x_unread = stage.tile([P, 2, ROWS, POS], BF16)
             x_neg_mean = small.tile([P, ROWS], F32)
-            for r in range(VECTOR_ROWS[b], ROWS):
+            for r in range(SCALAR_ROWS[b]):
                 nc.scalar.activation(
                     out=x_unread[:, 0, r, :], in_=x_row(b, r), func=ACT.Identity,
                     scale=-1.0 / POS, accum_out=x_neg_mean[:, r : r + 1],
                 )
-            for r in range(VECTOR_ROWS[b], ROWS):
+            for r in range(SCALAR_ROWS[b]):
                 nc.scalar.activation(
                     out=x_unread[:, 1, r, :], in_=x_row(b, r), func=ACT.Square,
                     bias=x_neg_mean[:, r : r + 1], accum_out=x_sum_sq[b][:, r : r + 1],
@@ -151,9 +162,9 @@ def tile_axialattentionblock_pa_kernel(
 
         def quantise_image(b):
             std = small.tile([P, ROWS], F32)
-            split = VECTOR_ROWS[b]
-            nc.scalar.activation(out=std[:, 0:split], in_=mean_var[b][:, 0:split, 1], func=ACT.Sqrt, scale=POS / (POS - 1.0))
-            nc.scalar.activation(out=std[:, split:ROWS], in_=x_sum_sq[b][:, split:ROWS], func=ACT.Sqrt, scale=1.0 / (POS - 1.0))
+            split = SCALAR_ROWS[b]
+            nc.scalar.activation(out=std[:, 0:split], in_=x_sum_sq[b][:, 0:split], func=ACT.Sqrt, scale=1.0 / (POS - 1.0))
+            nc.scalar.activation(out=std[:, split:ROWS], in_=mean_var[b][:, split:ROWS, 1], func=ACT.Sqrt, scale=POS / (POS - 1.0))
             padded = small.tile([P, ROWS], F32)
             nc.vector.tensor_scalar_add(out=padded[:], in0=std[:], scalar1=1e-8)
             recip = small.tile([P, ROWS], F32)
@@ -166,6 +177,13 @@ def tile_axialattentionblock_pa_kernel(
                     nc.vector.tensor_scalar_mul(
                         out=scaled[:, g, j * POS : (j + 1) * POS], in0=x_sb[b][:, g, j * POS : (j + 1) * POS],
                         scalar1=factor[:, g * PACK + j : g * PACK + j + 1],
+                    )
+            if b == 0:
+                keep_warm = psum.tile([P, POS], F32, name="v_bank", bufs=V_BANK_BUFS)
+                for r in range(ROWS):
+                    nc.tensor.matmul(
+                        out=keep_warm[:], lhsT=ones[:], rhs=scaled[:, r // PACK, (r % PACK) * POS : (r % PACK + 1) * POS],
+                        start=True, stop=True,
                     )
             grouped = []
             for g in range(PASSES):
@@ -192,22 +210,24 @@ def tile_axialattentionblock_pa_kernel(
             for pair in range(2):
                 tiles["qk_bank%d" % pair, n] = psum.tile([P, 2, QK, HEAD], F32, name="qk_bank%d" % pair)
             tiles["v_bank", n] = psum.tile([P, POS_TILES, HEAD], F32, name="v_bank", bufs=V_BANK_BUFS)
-            for t in range(POS_TILES):
+            qk_parts = [
+                (t, tiles["qk_bank%d" % (t // 2), n][:, t % 2].rearrange("p s c -> p (s c)"), slice(c0, c0 + QK * HEAD))
+                for t in range(POS_TILES)
+            ]
+            v_parts = [(t, tiles["v_bank", n][:, t, :], slice(c0 + QK * HEAD, c0 + 3 * HEAD)) for t in range(POS_TILES)]
+            parts = qk_parts + v_parts if n == 0 else [part for both in zip(qk_parts, v_parts) for part in both]
+            for t, acc, cols in parts:
                 positions = slice(t * P, (t + 1) * P)
-                for acc, cols in (
-                    (tiles["qk_bank%d" % (t // 2), n][:, t % 2].rearrange("p s c -> p (s c)"), slice(c0, c0 + QK * HEAD)),
-                    (tiles["v_bank", n][:, t, :], slice(c0 + QK * HEAD, c0 + 3 * HEAD)),
-                ):
-                    for g in range(PASSES):
-                        nc.tensor.matmul_mx(
-                            out=acc,
-                            lhsT=h_codes[b][:, g, positions].bitcast(FP8X4),
-                            lhsT_scale=h_planes[b][:, g, positions],
-                            rhs=w_words[:, g, cols].bitcast(FP8X4),
-                            rhs_scale=w_planes[:, g, cols],
-                            start=(g == 0),
-                            stop=(g == PASSES - 1),
-                        )
+                for g in range(PASSES):
+                    nc.tensor.matmul_mx(
+                        out=acc,
+                        lhsT=h_codes[b][:, g, positions].bitcast(FP8X4),
+                        lhsT_scale=h_planes[b][:, g, positions],
+                        rhs=w_words[:, g, cols].bitcast(FP8X4),
+                        rhs_scale=w_planes[:, g, cols],
+                        start=(g == 0),
+                        stop=(g == PASSES - 1),
+                    )
 
         def leave_psum(n):
             h = n % HEADS
@@ -219,7 +239,7 @@ def tile_axialattentionblock_pa_kernel(
             nc.sync.dma_start(out=dram_head(out_2, n), in_=v_out[:].rearrange("p t c -> p (t c)"))
             y = work.tile([P, QK, POS_TILES, HEAD], F32)
             sum_y = small.tile([P, QK, POS_TILES], F32)
-            for s, t in GROUPS:
+            for s, t in sorted(GROUPS, key=lambda group: group[1]) if n == 0 else GROUPS:
                 nc.scalar.activation(
                     out=y[:, s, t, :], in_=tiles["qk_bank%d" % (t // 2), n][:, t % 2, s, :], func=ACT.Copy,
                     accum_out=sum_y[:, s, t : t + 1],
@@ -288,10 +308,7 @@ def tile_axialattentionblock_pa_kernel(
         nc.scalar.activation(
             out=bias_unread[:], in_=bias_rows[:], func=ACT.Identity, scale=-1.0 / HEAD, accum_out=neg_mean_column[:],
         )
-        for i, bias_bank in enumerate(bias_banks):
-            nc.scalar.copy(
-                out=bias[:].rearrange("p h s c -> p (h s) c")[:, 8 * i : 8 * (i + 1), :], in_=bias_bank[:]
-            )
+        copy_bias_bank(0)
         spread = psum.tile([P, POS_TILES, HEAD], F32, name="v_bank", bufs=V_BANK_BUFS)
         nc.tensor.matmul(
             out=spread[:, 0, :], lhsT=neg_mean_column[:, 0:1].to_broadcast([P, P]), rhs=identity[:], start=True, stop=True,
@@ -302,12 +319,16 @@ def tile_axialattentionblock_pa_kernel(
         statistics_on_scalar(1)
         project(0)
         def pipeline_step(step):
+            if step in BIAS_STEPS:
+                spread_bias_bank(BIAS_STEPS[step])
             if step + 1 < UNITS:
                 project(step + 1)
             if 0 <= step - 2 < UNITS:
                 sum_squares(step - 2)
             if step < UNITS:
                 leave_psum(step)
+            if step in BIAS_STEPS:
+                copy_bias_bank(BIAS_STEPS[step])
             if 0 <= step - 2 < UNITS:
                 take_root(step - 2)
             if step >= 3:

@@ -27,8 +27,7 @@ GROUPS = [(s, t) for s in range(QK) for t in range(POS_TILES)]
 UNITS = BATCH * HEADS
 LOAD_COLUMNS = 2 * 3 * HEAD
 BIAS_GROUPS = OUT // HEAD
-BIAS_BANKS = 3
-BIAS_STEPS = {1: 1, 3: 2}
+EARLY_GROUPS = 8
 SCALAR_ROWS = (2, 4)
 IMAGE_0_PIECES = ((2, 1), (3, 1), (0, 2), (4, 2), (6, 2))
 
@@ -83,6 +82,9 @@ def tile_axialattentionblock_pa_kernel(
                     nc.sync.dma_start(out=ln_rows[0:1, 0, s, :], in_=w_vec.unsqueeze(0))
                     nc.sync.dma_start(out=ln_rows[0:1, 1, s, :], in_=b_vec.unsqueeze(0))
 
+        gain_x = keep.tile([P, ROWS], F32)
+        nc.gpsimd.tensor_copy(out=gain_x[:], in_=w1[:])
+
         w_planes = keep.tile([P, PASSES, OUT], U8, align_bytes=64)
         nc.vector.memset(w_planes[:].bitcast(I32), 0)
         scales_dram = qkv_w_scales.rearrange("g (i odd r) o -> odd r i g o", i=2, odd=2, r=4)
@@ -110,24 +112,17 @@ def tile_axialattentionblock_pa_kernel(
         identity_bf16 = keep.tile([P, P], BF16)
         make_identity(nc, identity_bf16[:])
         bias = keep.tile([P, HEADS, 3, HEAD], BF16)
-        bias_banks = {}
-
-        def spread_bias_bank(i):
-            bias_bank = psum.tile([P, BIAS_GROUPS // BIAS_BANKS, HEAD], BF16, name="v_bank", bufs=V_BANK_BUFS)
-            for r in range(BIAS_GROUPS // BIAS_BANKS):
-                row = i * (BIAS_GROUPS // BIAS_BANKS) + r
-                nc.tensor.matmul(
-                    out=bias_bank[:, r, :], lhsT=identity_bf16[:, row : row + 1].to_broadcast([P, P]),
-                    rhs=bias_rows[:], start=True, stop=True,
-                )
-            bias_banks[i] = bias_bank
-
-        def copy_bias_bank(i):
-            nc.scalar.copy(
-                out=bias[:].rearrange("p h s c -> p (h s) c")[:, 8 * i : 8 * (i + 1), :], in_=bias_banks[i][:]
+        bias_groups = bias[:].rearrange("p h s c -> p (h s) c")
+        nc.sync.dma_start(
+            out=bias_groups[:, EARLY_GROUPS:, :].rearrange("p r c -> p (r c)"),
+            in_=qkv_b[EARLY_GROUPS * HEAD :].partition_broadcast(P),
+        )
+        bias_bank = psum.tile([P, EARLY_GROUPS, HEAD], BF16, name="v_bank", bufs=V_BANK_BUFS)
+        for r in range(EARLY_GROUPS):
+            nc.tensor.matmul(
+                out=bias_bank[:, r, :], lhsT=identity_bf16[:, r : r + 1].to_broadcast([P, P]),
+                rhs=bias_rows[:], start=True, stop=True,
             )
-
-        spread_bias_bank(0)
         gain = ln_bank[:, 0]
         shift = ln_bank[:, 1]
 
@@ -169,14 +164,13 @@ def tile_axialattentionblock_pa_kernel(
             nc.vector.tensor_scalar_add(out=padded[:], in0=std[:], scalar1=1e-8)
             recip = small.tile([P, ROWS], F32)
             nc.vector.reciprocal(out=recip[:], in_=padded[:])
-            factor = small.tile([P, ROWS], F32)
-            nc.vector.tensor_tensor(out=factor[:], in0=recip[:], in1=w1[:], op=ALU.mult)
             scaled = stage.tile([P, PASSES, PACK * POS], BF16)
             for g in range(PASSES):
                 for j in range(PACK):
-                    nc.vector.tensor_scalar_mul(
+                    r = g * PACK + j
+                    nc.vector.tensor_scalar(
                         out=scaled[:, g, j * POS : (j + 1) * POS], in0=x_sb[b][:, g, j * POS : (j + 1) * POS],
-                        scalar1=factor[:, g * PACK + j : g * PACK + j + 1],
+                        scalar1=recip[:, r : r + 1], scalar2=gain_x[:, r : r + 1], op0=ALU.mult, op1=ALU.mult,
                     )
             if b == 0:
                 keep_warm = psum.tile([P, POS], F32, name="v_bank", bufs=V_BANK_BUFS)
@@ -308,7 +302,7 @@ def tile_axialattentionblock_pa_kernel(
         nc.scalar.activation(
             out=bias_unread[:], in_=bias_rows[:], func=ACT.Identity, scale=-1.0 / HEAD, accum_out=neg_mean_column[:],
         )
-        copy_bias_bank(0)
+        nc.scalar.copy(out=bias_groups[:, 0:EARLY_GROUPS, :], in_=bias_bank[:])
         spread = psum.tile([P, POS_TILES, HEAD], F32, name="v_bank", bufs=V_BANK_BUFS)
         nc.tensor.matmul(
             out=spread[:, 0, :], lhsT=neg_mean_column[:, 0:1].to_broadcast([P, P]), rhs=identity[:], start=True, stop=True,
@@ -319,16 +313,12 @@ def tile_axialattentionblock_pa_kernel(
         statistics_on_scalar(1)
         project(0)
         def pipeline_step(step):
-            if step in BIAS_STEPS:
-                spread_bias_bank(BIAS_STEPS[step])
             if step + 1 < UNITS:
                 project(step + 1)
             if 0 <= step - 2 < UNITS:
                 sum_squares(step - 2)
             if step < UNITS:
                 leave_psum(step)
-            if step in BIAS_STEPS:
-                copy_bias_bank(BIAS_STEPS[step])
             if 0 <= step - 2 < UNITS:
                 take_root(step - 2)
             if step >= 3:

@@ -198,6 +198,9 @@ def tile_axialattentionblock_pa_kernel(
 
         tiles = {}
 
+        def parts(n):
+            return ((0,), (1,)) if n == UNITS - 1 else ((0, 1),)
+
         def project(n):
             b, h = divmod(n, HEADS)
             c0 = h * 3 * HEAD
@@ -239,60 +242,69 @@ def tile_axialattentionblock_pa_kernel(
                     accum_out=sum_y[:, s, t : t + 1],
                 )
             neg_mean = small.tile([P, QK, POS_TILES], F32)
-            for s in range(QK):
-                nc.gpsimd.tensor_scalar(
-                    out=neg_mean[:, s, :], in0=sum_y[:, s, :], scalar1=-1.0 / HEAD,
-                    scalar2=neg_bias_mean[:, h, s : s + 1], op0=ALU.mult, op1=ALU.add,
-                )
             u = work.tile([P, QK, POS_TILES, HEAD], F32, bufs=U_BUFS)
-            nc.gpsimd.tensor_tensor(
-                out=u[:], in0=y[:],
-                in1=bias[:, h, 0:QK, :].unsqueeze(2).to_broadcast([P, QK, POS_TILES, HEAD]), op=ALU.add,
-            )
+            for part in parts(n):
+                for s in part:
+                    nc.gpsimd.tensor_scalar(
+                        out=neg_mean[:, s, :], in0=sum_y[:, s, :], scalar1=-1.0 / HEAD,
+                        scalar2=neg_bias_mean[:, h, s : s + 1], op0=ALU.mult, op1=ALU.add,
+                    )
+                both = slice(part[0], part[-1] + 1)
+                nc.gpsimd.tensor_tensor(
+                    out=u[:, both], in0=y[:, both],
+                    in1=bias[:, h, both, :].unsqueeze(2).to_broadcast([P, len(part), POS_TILES, HEAD]), op=ALU.add,
+                )
             tiles["u", n] = u
             tiles["neg_mean", n] = neg_mean
 
-        def sum_squares(n):
-            unread = work.tile([P, QK, POS_TILES, HEAD], BF16)
-            sum_sq = small.tile([P, QK, POS_TILES], F32)
-            for s, t in GROUPS:
-                nc.scalar.activation(
-                    out=unread[:, s, t, :], in_=tiles["u", n][:, s, t, :], func=ACT.Square,
-                    bias=tiles["neg_mean", n][:, s, t : t + 1], accum_out=sum_sq[:, s, t : t + 1],
-                )
-            tiles["sum_sq", n] = sum_sq
+        def sum_squares(n, part):
+            if part[0] == 0:
+                tiles["unread", n] = work.tile([P, QK, POS_TILES, HEAD], BF16, name="unread")
+                tiles["sum_sq", n] = small.tile([P, QK, POS_TILES], F32, name="sum_sq")
+            for s in part:
+                for t in range(POS_TILES):
+                    nc.scalar.activation(
+                        out=tiles["unread", n][:, s, t, :], in_=tiles["u", n][:, s, t, :], func=ACT.Square,
+                        bias=tiles["neg_mean", n][:, s, t : t + 1], accum_out=tiles["sum_sq", n][:, s, t : t + 1],
+                    )
 
-        def take_root(n):
-            ln_std = small.tile([P, QK, POS_TILES], F32)
+        def take_root(n, part):
+            if part[0] == 0:
+                tiles["ln_std", n] = small.tile([P, QK, POS_TILES], F32, name="ln_std")
+            both = slice(part[0], part[-1] + 1)
             nc.scalar.activation(
-                out=ln_std[:], in_=tiles["sum_sq", n][:], func=ACT.Sqrt, scale=1.0 / HEAD, bias=ln_eps[:, 0:1]
+                out=tiles["ln_std", n][:, both], in_=tiles["sum_sq", n][:, both], func=ACT.Sqrt, scale=1.0 / HEAD, bias=ln_eps[:, 0:1]
             )
-            tiles["ln_std", n] = ln_std
 
-        def centre(n):
-            centred = work.tile([P, QK, POS_TILES, HEAD], F32)
-            for s, t in GROUPS:
-                nc.vector.scalar_tensor_tensor(
-                    out=centred[:, s, t, :], in0=tiles["u", n][:, s, t, :], scalar=tiles["neg_mean", n][:, s, t : t + 1],
-                    in1=gain[:, s, :], op0=ALU.add, op1=ALU.mult,
+        def centre(n, part):
+            if part[0] == 0:
+                tiles["centred", n] = work.tile([P, QK, POS_TILES, HEAD], F32, name="centred")
+            for s in part:
+                for t in range(POS_TILES):
+                    nc.vector.scalar_tensor_tensor(
+                        out=tiles["centred", n][:, s, t, :], in0=tiles["u", n][:, s, t, :],
+                        scalar=tiles["neg_mean", n][:, s, t : t + 1], in1=gain[:, s, :], op0=ALU.add, op1=ALU.mult,
+                    )
+
+        def invert(n, part):
+            if part[0] == 0:
+                tiles["rstd", n] = small.tile([P, QK, POS_TILES], F32, name="rstd")
+            both = slice(part[0], part[-1] + 1)
+            nc.vector.reciprocal(out=tiles["rstd", n][:, both], in_=tiles["ln_std", n][:, both])
+
+        def finish(n, part):
+            if part[0] == 0:
+                tiles["qk_out", n] = work.tile([P, QK, POS_TILES, HEAD], F32, name="qk_out")
+            for s in part:
+                for t in range(POS_TILES):
+                    nc.vector.scalar_tensor_tensor(
+                        out=tiles["qk_out", n][:, s, t, :], in0=tiles["centred", n][:, s, t, :],
+                        scalar=tiles["rstd", n][:, s, t : t + 1], in1=shift[:, s, :], op0=ALU.mult, op1=ALU.add,
+                    )
+            for s in part:
+                nc.sync.dma_start(
+                    out=dram_head((out_0, out_1)[s], n), in_=tiles["qk_out", n][:, s].rearrange("p t c -> p (t c)")
                 )
-            tiles["centred", n] = centred
-
-        def invert(n):
-            rstd = small.tile([P, QK, POS_TILES], F32)
-            nc.vector.reciprocal(out=rstd[:], in_=tiles["ln_std", n][:])
-            tiles["rstd", n] = rstd
-
-        def finish(n):
-            rstd = tiles["rstd", n]
-            qk_out = work.tile([P, QK, POS_TILES, HEAD], F32)
-            for s, t in GROUPS:
-                nc.vector.scalar_tensor_tensor(
-                    out=qk_out[:, s, t, :], in0=tiles["centred", n][:, s, t, :], scalar=rstd[:, s, t : t + 1],
-                    in1=shift[:, s, :], op0=ALU.mult, op1=ALU.add,
-                )
-            for s, out in enumerate((out_0, out_1)):
-                nc.sync.dma_start(out=dram_head(out, n), in_=qk_out[:, s].rearrange("p t c -> p (t c)"))
 
         statistics_on_vector(0)
         statistics_on_scalar(0)
@@ -315,20 +327,39 @@ def tile_axialattentionblock_pa_kernel(
         def pipeline_step(step):
             if step + 1 < UNITS:
                 project(step + 1)
-            if 0 <= step - 2 < UNITS:
-                sum_squares(step - 2)
-            if step < UNITS:
-                leave_psum(step)
-            if 0 <= step - 2 < UNITS:
-                take_root(step - 2)
+            if step >= 2:
+                sum_squares(step - 2, (0, 1))
+            if step == UNITS - 1:
+                take_root(step - 2, (0, 1))
+            leave_psum(step)
+            if 2 <= step < UNITS - 1:
+                take_root(step - 2, (0, 1))
             if step >= 3:
-                invert(step - 3)
-            if 0 <= step - 2 < UNITS:
-                centre(step - 2)
+                invert(step - 3, (0, 1))
+            if step >= 2:
+                centre(step - 2, (0, 1))
             if step >= 3:
-                finish(step - 3)
+                finish(step - 3, (0, 1))
 
         pipeline_step(0)
         quantise_image(1)
-        for step in range(1, UNITS + 3):
+        for step in range(1, UNITS):
             pipeline_step(step)
+
+        q, k = parts(UNITS - 1)
+        sum_squares(UNITS - 2, (0, 1))
+        take_root(UNITS - 2, (0, 1))
+        for part in (q, k):
+            sum_squares(UNITS - 1, part)
+            take_root(UNITS - 1, part)
+        invert(UNITS - 3, (0, 1))
+        centre(UNITS - 2, (0, 1))
+        finish(UNITS - 3, (0, 1))
+        invert(UNITS - 2, (0, 1))
+        centre(UNITS - 1, q)
+        finish(UNITS - 2, (0, 1))
+        invert(UNITS - 1, q)
+        centre(UNITS - 1, k)
+        finish(UNITS - 1, q)
+        invert(UNITS - 1, k)
+        finish(UNITS - 1, k)

from contextlib import ExitStack

import concourse.mybir as mybir
from concourse.masks import make_identity

F32 = mybir.dt.float32
BF16 = mybir.dt.bfloat16
I32 = mybir.dt.int32
U32 = mybir.dt.uint32
U8 = mybir.dt.uint8
FP8X4 = mybir.dt.float8_e4m3fn_x4
ALU = mybir.AluOpType
ACT = mybir.ActivationFunctionType

P = 128
PACK = 4
PASSES = 2
BATCH = 2
POS = 512
POS_TILES = POS // P
HEADS = 8
HEAD = 128
OUT = HEADS * 3 * HEAD
ROWS = PASSES * PACK
QK = 2
GROUPS = [(s, t) for s in range(QK) for t in range(POS_TILES)]
UNITS = BATCH * HEADS
LOAD_COLUMNS = 2 * 3 * HEAD
BIAS_GROUPS = OUT // HEAD
EARLY_GROUPS = 8
SCALAR_ROWS = (2, 4)
IMAGE_0_PIECES = ((2, 1), (3, 1), (0, 2), (4, 2), (6, 2))

STAGE_BUFS = 2
SMALL_BUFS = 6
WORK_BUFS = 3
U_BUFS = 5
BANK_BUFS = 2
V_BANK_BUFS = 3

FLOPS = 2 * BATCH * POS * (PASSES * P * PACK) * OUT


def tile_axialattentionblock_pa_kernel(
    tc, x, norm1_w, qkv_w_words, qkv_w_scales, qkv_b, qn_w, qn_b, kn_w, kn_b, out_0, out_1, out_2
):
    nc = tc.nc
    with ExitStack() as stack:
        keep = stack.enter_context(tc.tile_pool(name="keep", bufs=1))
        stage = stack.enter_context(tc.tile_pool(name="stage", bufs=STAGE_BUFS))
        small = stack.enter_context(tc.tile_pool(name="small", bufs=SMALL_BUFS))
        work = stack.enter_context(tc.tile_pool(name="work", bufs=WORK_BUFS))
        psum = stack.enter_context(tc.psum_pool(name="psum", bufs=BANK_BUFS))
        const_psum = stack.enter_context(tc.psum_pool(name="const_psum", bufs=1))
        stack.enter_context(tc.manual_schedule())

        ln_eps = keep.tile([P, 1], F32)
        nc.vector.memset(ln_eps[:], 1e-5)
        warm = keep.tile([P, 1], F32)
        nc.scalar.activation(out=warm[:], in_=ln_eps[:], func=ACT.Sqrt)

        ln_rows = keep.tile([P, 2, QK, HEAD], BF16)
        nc.vector.memset(ln_rows[:], 0.0)
        ones = keep.tile([P, P], BF16)
        nc.vector.memset(ones[:], 1.0)
        bias_rows = keep.tile([P, HEAD], BF16)
        nc.vector.memset(bias_rows[:], 0.0)
        x_dram = x.rearrange("b (g p j) hh ww -> b g p (j hh ww)", g=PASSES, p=P, j=PACK)
        x_sb = [keep.tile([P, PASSES, PACK * POS], BF16, name="x_sb%d" % b) for b in range(BATCH)]
        w1 = keep.tile([P, ROWS], BF16)
        for b in range(BATCH):
            for r, count in IMAGE_0_PIECES if b == 0 else ((0, PACK), (PACK, PACK)):
                columns = slice((r % PACK) * POS, (r % PACK + count) * POS)
                nc.sync.dma_start(out=x_sb[b][:, r // PACK, columns], in_=x_dram[b, r // PACK][:, columns])
            if b == 0:
                nc.sync.dma_start(
                    out=w1[:].rearrange("p (g j) -> p g j", g=PASSES),
                    in_=norm1_w.rearrange("(g p j) -> p g j", g=PASSES, p=P, j=PACK),
                )
                nc.sync.dma_start(out=bias_rows[0:BIAS_GROUPS, :], in_=qkv_b.rearrange("(r c) -> r c", c=HEAD))
                for s, (w_vec, b_vec) in enumerate(((qn_w, qn_b), (kn_w, kn_b))):
                    nc.sync.dma_start(out=ln_rows[0:1, 0, s, :], in_=w_vec.unsqueeze(0))
                    nc.sync.dma_start(out=ln_rows[0:1, 1, s, :], in_=b_vec.unsqueeze(0))

        gain_x = keep.tile([P, ROWS], F32)
        nc.gpsimd.tensor_copy(out=gain_x[:], in_=w1[:])

        w_planes = keep.tile([P, PASSES, OUT], U8, align_bytes=64)
        nc.vector.memset(w_planes[:].bitcast(I32), 0)
        scales_dram = qkv_w_scales.rearrange("g (i odd r) o -> odd r i g o", i=2, odd=2, r=4)
        for odd in range(2):
            for r in range(4):
                nc.sync.dma_start(
                    out=w_planes[32 * odd + r : P : 64].bitcast(I32), in_=scales_dram[odd, r].bitcast(I32)
                )

        w_words = keep.tile([P, PASSES, OUT], U32, align_bytes=64)
        words_dram = qkv_w_words.rearrange("g p o e -> p g (o e)")
        for c0 in range(0, OUT, LOAD_COLUMNS):
            nc.sync.dma_start(
                out=w_words[:, :, c0 : c0 + LOAD_COLUMNS].bitcast(I32),
                in_=words_dram[:, :, PACK * c0 : PACK * (c0 + LOAD_COLUMNS)].bitcast(I32),
            )

        identity = keep.tile([P, P], F32)
        make_identity(nc, identity[:])
        ln_bank = const_psum.tile([P, 2, QK, HEAD], F32)
        nc.tensor.matmul(
            out=ln_bank[:].rearrange("p v s c -> p (v s c)"), lhsT=ones[:],
            rhs=ln_rows[:].rearrange("p v s c -> p (v s c)"), start=True, stop=True,
        )
        identity_bf16 = keep.tile([P, P], BF16)
        make_identity(nc, identity_bf16[:])
        bias = keep.tile([P, HEADS, 3, HEAD], BF16)
        bias_groups = bias[:].rearrange("p h s c -> p (h s) c")
        nc.sync.dma_start(
            out=bias_groups[:, EARLY_GROUPS:, :].rearrange("p r c -> p (r c)"),
            in_=qkv_b[EARLY_GROUPS * HEAD :].partition_broadcast(P),
        )
        bias_bank = psum.tile([P, EARLY_GROUPS, HEAD], BF16, name="v_bank", bufs=V_BANK_BUFS)
        for r in range(EARLY_GROUPS):
            nc.tensor.matmul(
                out=bias_bank[:, r, :], lhsT=identity_bf16[:, r : r + 1].to_broadcast([P, P]),
                rhs=bias_rows[:], start=True, stop=True,
            )
        gain = ln_bank[:, 0]
        shift = ln_bank[:, 1]

        h_codes = [keep.tile([P, PASSES, POS], U32, name="h_codes%d" % b, align_bytes=64) for b in range(BATCH)]
        h_planes = [keep.tile([P, PASSES, POS], U8, name="h_planes%d" % b, align_bytes=64) for b in range(BATCH)]
        mean_var = [keep.tile([P, ROWS, 2], F32, name="mean_var%d" % b) for b in range(BATCH)]
        x_sum_sq = [keep.tile([P, ROWS], F32, name="x_sum_sq%d" % b) for b in range(BATCH)]

        def x_row(b, r):
            return x_sb[b][:, r // PACK, (r % PACK) * POS : (r % PACK + 1) * POS]

        def statistics_on_vector(b):
            stats = small.tile([P, ROWS, 6], F32)
            for r in range(SCALAR_ROWS[b], ROWS):
                nc.vector.bn_stats(out=stats[:, r, :], in_=x_row(b, r))
            for r in range(SCALAR_ROWS[b], ROWS):
                nc.vector.bn_aggr(out=mean_var[b][:, r, :], in_=stats[:, r, :])

        def statistics_on_scalar(b):
            x_unread = stage.tile([P, 2, ROWS, POS], BF16)
            x_neg_mean = small.tile([P, ROWS], F32)
            for r in range(SCALAR_ROWS[b]):
                nc.scalar.activation(
                    out=x_unread[:, 0, r, :], in_=x_row(b, r), func=ACT.Identity,
                    scale=-1.0 / POS, accum_out=x_neg_mean[:, r : r + 1],
                )
            for r in range(SCALAR_ROWS[b]):
                nc.scalar.activation(
                    out=x_unread[:, 1, r, :], in_=x_row(b, r), func=ACT.Square,
                    bias=x_neg_mean[:, r : r + 1], accum_out=x_sum_sq[b][:, r : r + 1],
                )

        def quantise_image(b):
            std = small.tile([P, ROWS], F32)
            split = SCALAR_ROWS[b]
            nc.scalar.activation(out=std[:, 0:split], in_=x_sum_sq[b][:, 0:split], func=ACT.Sqrt, scale=1.0 / (POS - 1.0))
            nc.scalar.activation(out=std[:, split:ROWS], in_=mean_var[b][:, split:ROWS, 1], func=ACT.Sqrt, scale=POS / (POS - 1.0))
            padded = small.tile([P, ROWS], F32)
            nc.vector.tensor_scalar_add(out=padded[:], in0=std[:], scalar1=1e-8)
            recip = small.tile([P, ROWS], F32)
            nc.vector.reciprocal(out=recip[:], in_=padded[:])
            scaled = stage.tile([P, PASSES, PACK * POS], BF16)
            for g in range(PASSES):
                for j in range(PACK):
                    r = g * PACK + j
                    nc.vector.tensor_scalar(
                        out=scaled[:, g, j * POS : (j + 1) * POS], in0=x_sb[b][:, g, j * POS : (j + 1) * POS],
                        scalar1=recip[:, r : r + 1], scalar2=gain_x[:, r : r + 1], op0=ALU.mult, op1=ALU.mult,
                    )
            if b == 0:
                keep_warm = psum.tile([P, POS], F32, name="v_bank", bufs=V_BANK_BUFS)
                for r in range(ROWS):
                    nc.tensor.matmul(
                        out=keep_warm[:], lhsT=ones[:], rhs=scaled[:, r // PACK, (r % PACK) * POS : (r % PACK + 1) * POS],
                        start=True, stop=True,
                    )
            grouped = []
            for g in range(PASSES):
                grouped.append(stage.tile([P, POS, PACK], BF16, name="grouped%d" % g, align_bytes=64))
                nc.vector.tensor_copy(
                    out=grouped[g][:].rearrange("p (t m) j -> p m j t", t=POS_TILES),
                    in_=scaled[:, g, :].rearrange("p (j m t) -> p m j t", j=PACK, t=POS_TILES),
                )
            for g in range(PASSES):
                nc.vector.quantize_mx(
                    out=h_codes[b][:, g, :].bitcast(FP8X4),
                    scales=h_planes[b][:, g, :],
                    in_=grouped[g][:].rearrange("p c j -> p (c j)"),
                )

        def dram_head(out, n):
            return out.rearrange("b h hh ww c -> (b h) (hh ww c)")[n].rearrange("(m f) -> m f", m=P)

        tiles = {}

        def parts(n):
            return ((0,), (1,)) if n == UNITS - 1 else ((0, 1),)

        def project(n):
            b, h = divmod(n, HEADS)
            c0 = h * 3 * HEAD
            for pair in range(2):
                tiles["qk_bank%d" % pair, n] = psum.tile([P, 2, QK, HEAD], F32, name="qk_bank%d" % pair)
            tiles["v_bank", n] = psum.tile([P, POS_TILES, HEAD], F32, name="v_bank", bufs=V_BANK_BUFS)
            qk_parts = [
                (t, tiles["qk_bank%d" % (t // 2), n][:, t % 2].rearrange("p s c -> p (s c)"), slice(c0, c0 + QK * HEAD))
                for t in range(POS_TILES)
            ]
            v_parts = [(t, tiles["v_bank", n][:, t, :], slice(c0 + QK * HEAD, c0 + 3 * HEAD)) for t in range(POS_TILES)]
            parts = qk_parts + v_parts if n == 0 else [part for both in zip(qk_parts, v_parts) for part in both]
            for t, acc, cols in parts:
                positions = slice(t * P, (t + 1) * P)
                for g in range(PASSES):
                    nc.tensor.matmul_mx(
                        out=acc,
                        lhsT=h_codes[b][:, g, positions].bitcast(FP8X4),
                        lhsT_scale=h_planes[b][:, g, positions],
                        rhs=w_words[:, g, cols].bitcast(FP8X4),
                        rhs_scale=w_planes[:, g, cols],
                        start=(g == 0),
                        stop=(g == PASSES - 1),
                    )

        def leave_psum(n):
            h = n % HEADS
            v_out = work.tile([P, POS_TILES, HEAD], F32)
            nc.vector.tensor_tensor(
                out=v_out[:], in0=tiles["v_bank", n][:],
                in1=bias[:, h, 2, :].unsqueeze(1).to_broadcast([P, POS_TILES, HEAD]), op=ALU.add,
            )
            nc.sync.dma_start(out=dram_head(out_2, n), in_=v_out[:].rearrange("p t c -> p (t c)"))
            y = work.tile([P, QK, POS_TILES, HEAD], F32)
            sum_y = small.tile([P, QK, POS_TILES], F32)
            for s, t in sorted(GROUPS, key=lambda group: group[1]) if n == 0 else GROUPS:
                nc.scalar.activation(
                    out=y[:, s, t, :], in_=tiles["qk_bank%d" % (t // 2), n][:, t % 2, s, :], func=ACT.Copy,
                    accum_out=sum_y[:, s, t : t + 1],
                )
            neg_mean = small.tile([P, QK, POS_TILES], F32)
            u = work.tile([P, QK, POS_TILES, HEAD], F32, bufs=U_BUFS)
            for part in parts(n):
                for s in part:
                    nc.gpsimd.tensor_scalar(
                        out=neg_mean[:, s, :], in0=sum_y[:, s, :], scalar1=-1.0 / HEAD,
                        scalar2=neg_bias_mean[:, h, s : s + 1], op0=ALU.mult, op1=ALU.add,
                    )
                both = slice(part[0], part[-1] + 1)
                nc.gpsimd.tensor_tensor(
                    out=u[:, both], in0=y[:, both],
                    in1=bias[:, h, both, :].unsqueeze(2).to_broadcast([P, len(part), POS_TILES, HEAD]), op=ALU.add,
                )
            tiles["u", n] = u
            tiles["neg_mean", n] = neg_mean

        def sum_squares(n, part):
            if part[0] == 0:
                tiles["unread", n] = work.tile([P, QK, POS_TILES, HEAD], BF16, name="unread")
                tiles["sum_sq", n] = small.tile([P, QK, POS_TILES], F32, name="sum_sq")
            for s in part:
                for t in range(POS_TILES):
                    nc.scalar.activation(
                        out=tiles["unread", n][:, s, t, :], in_=tiles["u", n][:, s, t, :], func=ACT.Square,
                        bias=tiles["neg_mean", n][:, s, t : t + 1], accum_out=tiles["sum_sq", n][:, s, t : t + 1],
                    )

        def take_root(n, part):
            if part[0] == 0:
                tiles["ln_std", n] = small.tile([P, QK, POS_TILES], F32, name="ln_std")
            both = slice(part[0], part[-1] + 1)
            nc.scalar.activation(
                out=tiles["ln_std", n][:, both], in_=tiles["sum_sq", n][:, both], func=ACT.Sqrt, scale=1.0 / HEAD, bias=ln_eps[:, 0:1]
            )

        def centre(n, part):
            if part[0] == 0:
                tiles["centred", n] = work.tile([P, QK, POS_TILES, HEAD], F32, name="centred")
            for s in part:
                for t in range(POS_TILES):
                    nc.vector.scalar_tensor_tensor(
                        out=tiles["centred", n][:, s, t, :], in0=tiles["u", n][:, s, t, :],
                        scalar=tiles["neg_mean", n][:, s, t : t + 1], in1=gain[:, s, :], op0=ALU.add, op1=ALU.mult,
                    )

        def invert(n, part):
            if part[0] == 0:
                tiles["rstd", n] = small.tile([P, QK, POS_TILES], F32, name="rstd")
            both = slice(part[0], part[-1] + 1)
            nc.vector.reciprocal(out=tiles["rstd", n][:, both], in_=tiles["ln_std", n][:, both])

        def finish(n, part):
            if part[0] == 0:
                tiles["qk_out", n] = work.tile([P, QK, POS_TILES, HEAD], F32, name="qk_out")
            for s in part:
                for t in range(POS_TILES):
                    nc.vector.scalar_tensor_tensor(
                        out=tiles["qk_out", n][:, s, t, :], in0=tiles["centred", n][:, s, t, :],
                        scalar=tiles["rstd", n][:, s, t : t + 1], in1=shift[:, s, :], op0=ALU.mult, op1=ALU.add,
                    )
            for s in part:
                nc.sync.dma_start(
                    out=dram_head((out_0, out_1)[s], n), in_=tiles["qk_out", n][:, s].rearrange("p t c -> p (t c)")
                )

        statistics_on_vector(0)
        statistics_on_scalar(0)
        quantise_image(0)
        bias_unread = keep.tile([P, HEAD], BF16)
        neg_mean_column = keep.tile([P, 1], F32)
        nc.scalar.activation(
            out=bias_unread[:], in_=bias_rows[:], func=ACT.Identity, scale=-1.0 / HEAD, accum_out=neg_mean_column[:],
        )
        nc.scalar.copy(out=bias_groups[:, 0:EARLY_GROUPS, :], in_=bias_bank[:])
        spread = psum.tile([P, POS_TILES, HEAD], F32, name="v_bank", bufs=V_BANK_BUFS)
        nc.tensor.matmul(
            out=spread[:, 0, :], lhsT=neg_mean_column[:, 0:1].to_broadcast([P, P]), rhs=identity[:], start=True, stop=True,
        )
        neg_bias_mean = keep.tile([P, HEADS, 3], F32)
        nc.vector.tensor_copy(out=neg_bias_mean[:].rearrange("p h s -> p (h s)"), in_=spread[:, 0, 0:BIAS_GROUPS])
        statistics_on_vector(1)
        statistics_on_scalar(1)
        project(0)
        def pipeline_step(step):
            if step + 1 < UNITS:
                project(step + 1)
            if step >= 2:
                sum_squares(step - 2, (0, 1))
            if step == UNITS - 1:
                take_root(step - 2, (0, 1))
            leave_psum(step)
            if 2 <= step < UNITS - 1:
                take_root(step - 2, (0, 1))
            if step >= 3:
                invert(step - 3, (0, 1))
            if step >= 2:
                centre(step - 2, (0, 1))
            if step >= 3:
                finish(step - 3, (0, 1))

        pipeline_step(0)
        quantise_image(1)
        for step in range(1, UNITS):
            pipeline_step(step)

        q, k = parts(UNITS - 1)
        sum_squares(UNITS - 2, (0, 1))
        take_root(UNITS - 2, (0, 1))
        for part in (q, k):
            sum_squares(UNITS - 1, part)
            take_root(UNITS - 1, part)
        invert(UNITS - 3, (0, 1))
        centre(UNITS - 2, (0, 1))
        finish(UNITS - 3, (0, 1))
        invert(UNITS - 2, (0, 1))
        centre(UNITS - 1, q)
        finish(UNITS - 2, (0, 1))
        invert(UNITS - 1, q)
        centre(UNITS - 1, k)
        finish(UNITS - 1, q)
        invert(UNITS - 1, k)
        finish(UNITS - 1, k)
